import numpy as np
import ml_dtypes


def mxq(x, axis, fmt="e4m3"):
    dtype, down = {"e4m3": (ml_dtypes.float8_e4m3fn, 7), "e5m2": (ml_dtypes.float8_e5m2, 14)}[fmt]
    v = np.moveaxis(np.asarray(x, np.float32).astype(ml_dtypes.bfloat16).astype(np.float64), axis, -1)
    blocks = v.reshape(v.shape[:-1] + (-1, 32))
    amax = np.abs(blocks).max(-1, keepdims=True)
    byte = np.maximum(np.where(amax > 0, np.frexp(amax)[1] - 1 + 127, 0) - down, 1)
    scale = np.exp2(byte - 127.0)
    codes = (blocks / scale).astype(np.float32).astype(dtype).astype(np.float64)
    return np.moveaxis((codes * scale).reshape(v.shape), -1, axis)


WIDE = False


def mx_kscale(k):
    if not WIDE:
        return np.ones(k)
    levels = np.array([10, -10, 5, -5, 0])
    a = np.random.permutation(np.resize(levels, k // 512 * 4)).reshape(k // 512, 4)
    idx = np.arange(k)
    return np.exp2(a[idx // 512, idx % 128 // 32])


BF16 = ml_dtypes.bfloat16


def bf(x):
    return np.asarray(x, np.float32).astype(BF16)


def f64(x):
    return np.asarray(x).astype(np.float64)


E2M1 = np.array([0.0, 0.5, 1.0, 1.5, 2.0, 3.0, 4.0, 6.0, -0.0, -0.5, -1.0, -1.5, -2.0, -3.0, -4.0, -6.0])


def pack_weight(w, fmt):
    k, n = w.shape
    w = f64(bf(w)).reshape(k // 32, 32, n)
    amax = np.abs(w).max(1)
    if fmt == "e4m3":
        byte = np.frexp(amax)[1] - 1 + 127 - 7
    else:
        mant, ex = np.frexp(amax / 6.0)
        byte = np.where(mant > 0.5, ex, ex - 1) + 127
    byte = np.clip(np.where(amax > 0, byte, 1), 1, 254)
    scaled = (w * np.exp2(127.0 - byte)[:, None, :]).reshape(k, n).astype(np.float32)
    by_word = np.ascontiguousarray(scaled.reshape(k // 512, 128, 4, n).transpose(0, 1, 3, 2))
    if fmt == "e4m3":
        words = by_word.astype(ml_dtypes.float8_e4m3fn).view(np.uint8)
    else:
        c = by_word.astype(ml_dtypes.float4_e2m1fn).view(np.uint8) & 0xF
        words = c[..., 0::2] | (c[..., 1::2] << 4)
    return np.ascontiguousarray(words), np.ascontiguousarray(byte.astype(np.uint8).reshape(k // 512, 16, n))


def unpack_weight(words, scales, fmt):
    g, p, n, _ = words.shape
    if fmt == "e4m3":
        vals = np.ascontiguousarray(words).view(ml_dtypes.float8_e4m3fn).astype(np.float64)
    else:
        nib = np.empty((g, p, n, 4), np.uint8)
        nib[..., 0::2] = words & 0xF
        nib[..., 1::2] = words >> 4
        vals = E2M1[nib]
    vals = vals * np.repeat(np.exp2(scales.astype(np.float64) - 127.0), 8, axis=1)[..., None]
    return vals.transpose(0, 1, 3, 2).reshape(g * 512, n)


B, IN, H, Z, G = 512, 1024, 1024, 256, 4
EPS = 1e-5


def sigmoid(v):
    return 1.0 / (1.0 + np.exp(-v))


def setup_inputs():
    s = mx_kscale(H)
    h = bf(np.random.standard_normal((B, H)) * s)
    c = bf(np.random.standard_normal((B, H)))
    zh = bf(np.random.standard_normal((B, G, Z)))
    zb = bf(np.random.standard_normal((B, G, Z)))
    px = bf(np.random.standard_normal((B, G, H)))
    dh_w = bf(np.random.standard_normal((G, H, Z)) / np.sqrt(Z))
    db_w = bf(np.random.standard_normal((G, H, Z)) / np.sqrt(Z))
    db_b = bf(np.random.standard_normal((G, H)) * 0.3)
    w_h = np.random.standard_normal((G, H, H)) / np.sqrt(H) / s
    cat = np.ascontiguousarray(w_h.swapaxes(1, 2)).reshape(-1, H)
    w_h_words, w_h_scales = pack_weight(cat, "e4m3")
    ln_w = bf(1.0 + np.random.standard_normal((G, H)) * 0.2)
    ln_b = bf(np.random.standard_normal((G, H)) * 0.3)
    return {"h": h,
            "c": c,
            "zh": zh,
            "zb": zb,
            "px": px,
            "dh_w": dh_w,
            "db_w": db_w,
            "db_b": db_b,
            "w_h_words": w_h_words,
            "w_h_scales": w_h_scales,
            "ln_w": ln_w,
            "ln_b": ln_b}


def reference(h, c, zh, zb, px, dh_w, db_w, db_b, w_h_words, w_h_scales, ln_w, ln_b):
    d_h = (f64(zh).transpose(1, 0, 2) @ f64(dh_w).transpose(0, 2, 1)).transpose(1, 0, 2)
    d_b = (f64(zb).transpose(1, 0, 2) @ f64(db_w).transpose(0, 2, 1)).transpose(1, 0, 2) + f64(db_b)[None]
    wh = (mxq(f64(h), 1, "e4m3") @ unpack_weight(w_h_words, w_h_scales, "e4m3").reshape(G, H, H).swapaxes(1, 2).reshape(G * H, H).T).reshape(B, G, H)
    y = d_h * wh + f64(px) + d_b
    mu = y.mean(-1, keepdims=True)
    var = y.var(-1, keepdims=True)
    yn = (y - mu) * (1.0 / np.sqrt(var + EPS)) * f64(ln_w)[None] + f64(ln_b)[None]
    i, f, g, o = yn[:, 0], yn[:, 1], yn[:, 2], yn[:, 3]
    c_next = sigmoid(f) * f64(c) + sigmoid(i) * np.tanh(g)
    h_next = sigmoid(o) * np.tanh(c_next)
    return (h_next, c_next)

@@ -1,0 +1,239 @@
+from contextlib import ExitStack
+
+import concourse.mybir as mybir
+from concourse.masks import make_identity
+
+F32 = mybir.dt.float32
+BF16 = mybir.dt.bfloat16
+I32 = mybir.dt.int32
+U32 = mybir.dt.uint32
+U8 = mybir.dt.uint8
+FP8X4 = mybir.dt.float8_e4m3fn_x4
+ALU = mybir.AluOpType
+ACT = mybir.ActivationFunctionType
+
+P = 128
+B, H, Z, G = 512, 1024, 256, 4
+EPS = 1e-5
+NBT = B // P
+BANK = 512
+HALVES = H // BANK
+K_PASS = 512
+PASSES = H // K_PASS
+PLANES = 4
+
+FLOPS = 2 * B * G * H * (H + 2 * Z)
+
+GATE_FUNC = (ACT.Sigmoid, ACT.Sigmoid, ACT.Tanh, ACT.Sigmoid)
+
+
+def tile_metalstmcell_pb_e_kernel(
+    tc, h, c, zh, zb, px, dh_w, db_w, db_b, w_h_words, w_h_scales, ln_w, ln_b, h_next, c_next
+):
+    nc = tc.nc
+    with ExitStack() as ctx:
+        const = ctx.enter_context(tc.tile_pool(name="const", bufs=1))
+        raw = ctx.enter_context(tc.tile_pool(name="raw", bufs=NBT))
+        gatew = ctx.enter_context(tc.tile_pool(name="gatew", bufs=2))
+        work = ctx.enter_context(tc.tile_pool(name="work", bufs=2))
+        stats = ctx.enter_context(tc.tile_pool(name="stats", bufs=4))
+        psum_t = ctx.enter_context(tc.psum_pool(name="psum_t", bufs=2))
+        psum_m = ctx.enter_context(tc.psum_pool(name="psum_m", bufs=2))
+
+        planes = const.tile([P, 8 // PLANES, H], U8, align_bytes=64)
+        nc.vector.memset(planes[:].bitcast(I32), 0)
+        ident_f32 = const.tile([P, P], F32)
+        make_identity(nc, ident_f32[:])
+        ident_bf16 = const.tile([P, P], BF16)
+        make_identity(nc, ident_bf16[:])
+        neg_half = const.tile([P, 1], F32)
+        nc.gpsimd.memset(neg_half[:], -0.5)
+
+        h_codes = const.tile([P, NBT, PASSES * P], U32, align_bytes=64)
+        h_scales = const.tile([P, NBT, PASSES * P], U8, align_bytes=64)
+        zhT = const.tile([P, NBT, G, P, 2], BF16)
+        zbT = const.tile([P, NBT, G, P, 2], BF16)
+        c_sb = const.tile([P, NBT, H], BF16)
+        keep_a = const.tile([P, NBT, H], F32)
+        keep_b = const.tile([P, NBT, H], F32)
+
+        def load_scale_planes(j):
+            for q in range(4):
+                nc.sync.dma_start(
+                    out=planes[32 * q : 32 * q + 4 * PLANES, j, :].bitcast(I32),
+                    in_=w_h_scales[PLANES * j : PLANES * (j + 1), 4 * q : 4 * q + 4, :].bitcast(I32),
+                )
+
+        def load_batch_tile(bt):
+            rows = slice(bt * P, (bt + 1) * P)
+            h_raw = raw.tile([P, H], BF16, tag="h_raw")
+            nc.sync.dma_start(out=h_raw[:], in_=h[rows, :])
+            zh_raw = raw.tile([P, G, Z], BF16, tag="zh_raw")
+            nc.sync.dma_start(out=zh_raw[:], in_=zh[rows])
+            zb_raw = raw.tile([P, G, Z], BF16, tag="zb_raw")
+            nc.sync.dma_start(out=zb_raw[:], in_=zb[rows])
+            return h_raw, zh_raw, zb_raw
+
+        def load_gate(g):
+            dh_raw = gatew.tile([P, H // P, Z], BF16, tag="dh_raw")
+            nc.sync.dma_start(out=dh_raw[:], in_=dh_w[g].rearrange("(nt p) z -> p nt z", p=P))
+            db_raw = gatew.tile([P, H // P, Z], BF16, tag="db_raw")
+            nc.sync.dma_start(out=db_raw[:], in_=db_w[g].rearrange("(nt p) z -> p nt z", p=P))
+            words = gatew.tile([P, PASSES, H], U32, tag="words", align_bytes=64)
+            nc.sync.dma_start(
+                out=words[:].bitcast(I32),
+                in_=w_h_words[PASSES * g : PASSES * (g + 1)]
+                .rearrange("s p n t -> p s (n t)")
+                .bitcast(I32),
+            )
+            px_sb = gatew.tile([P, NBT, H], BF16, tag="px_sb")
+            nc.sync.dma_start(out=px_sb[:], in_=px[:, g, :].rearrange("(bt p) n -> p bt n", p=P))
+            beta = gatew.tile([P, H], BF16, tag="beta")
+            nc.sync.dma_start(out=beta[:], in_=db_b[g].partition_broadcast(P))
+            lnw = gatew.tile([P, H], BF16, tag="lnw")
+            nc.sync.dma_start(out=lnw[:], in_=ln_w[g].partition_broadcast(P))
+            lnb = gatew.tile([P, H], BF16, tag="lnb")
+            nc.sync.dma_start(out=lnb[:], in_=ln_b[g].partition_broadcast(P))
+            return dh_raw, db_raw, words, px_sb, beta, lnw, lnb
+
+        def transpose_pairs(word_blocks, dst):
+            tp = psum_t.tile([P, 4, P], F32, tag="tp")
+            for j in range(4):
+                nc.tensor.transpose(tp[:, j, :], word_blocks[:, j, :], ident_f32[:])
+            nc.scalar.copy(out=dst, in_=tp[:].bitcast(BF16))
+
+        def prepare_batch_tile(bt, h_raw, zh_raw, zb_raw):
+            transpose_pairs(zh_raw[:].bitcast(F32), zhT[:, bt].rearrange("p g b e -> p g (b e)"))
+            transpose_pairs(zb_raw[:].bitcast(F32), zbT[:, bt].rearrange("p g b e -> p g (b e)"))
+            h_words = h_raw[:].bitcast(F32)
+            tp = psum_t.tile([P, 4, P], F32, tag="tp")
+            for s in range(PASSES):
+                for u in range(2):
+                    nc.tensor.transpose(
+                        tp[:, 2 * s + u, :],
+                        h_words[:, 256 * s + u : 256 * (s + 1) : 2],
+                        ident_f32[:],
+                    )
+            grouped = raw.tile([P, PASSES, P, 4], BF16, tag="grouped", bufs=2, align_bytes=64)
+            nc.vector.tensor_copy(
+                out=grouped[:].bitcast(F32), in_=tp[:].rearrange("p (s u) b -> p s b u", u=2)
+            )
+            nc.vector.quantize_mx(
+                out=h_codes[:, bt, :].bitcast(FP8X4),
+                scales=h_scales[:, bt, :],
+                in_=grouped[:].rearrange("p s b t -> p (s b t)"),
+            )
+
+        def prepare_gate(dh_raw, db_raw):
+            dhT = gatew.tile([P, H, 2], BF16, tag="dhT")
+            dbT = gatew.tile([P, H, 2], BF16, tag="dbT")
+            for src, dst in ((dh_raw, dhT), (db_raw, dbT)):
+                src_words = src[:].bitcast(F32)
+                dst_blocks = dst[:].rearrange("p (nt r) e -> p nt (r e)", r=P)
+                for q in range(H // P // 4):
+                    transpose_pairs(src_words[:, 4 * q : 4 * q + 4, :], dst_blocks[:, 4 * q : 4 * q + 4, :])
+            return dhT, dbT
+
+        def gate_preactivation(g, bt, dhT, dbT, words, px_sb, beta, lnw, lnb):
+            a_sb = work.tile([P, H], F32, tag="a_sb")
+            t = work.tile([P, H], F32, tag="t")
+            y = work.tile([P, H], F32, tag="y", bufs=3)
+            ysum = stats.tile([P, HALVES], F32, tag="ysum")
+            d_banks = []
+            for half in range(HALVES):
+                cols = slice(half * BANK, (half + 1) * BANK)
+                a_ps = psum_m.tile([P, BANK], F32, tag="a_ps")
+                for e in range(2):
+                    nc.tensor.matmul(
+                        a_ps[:], lhsT=zhT[:, bt, g, :, e], rhs=dhT[:, cols, e], start=(e == 0), stop=(e == 1)
+                    )
+                w_ps = psum_m.tile([P, BANK], F32, tag="w_ps")
+                for s in range(PASSES):
+                    group = PASSES * g + s
+                    row0 = 4 * (group % PLANES)
+                    nc.tensor.matmul_mx(
+                        out=w_ps[:],
+                        lhsT=h_codes[:, bt, s * P : (s + 1) * P].bitcast(FP8X4),
+                        lhsT_scale=h_scales[:, bt, s * P : (s + 1) * P],
+                        rhs=words[:, s, cols].bitcast(FP8X4),
+                        rhs_scale=planes[row0:P, group // PLANES, cols],
+                        start=(s == 0),
+                        stop=(s == PASSES - 1),
+                    )
+                d_ps = psum_m.tile([P, BANK], F32, tag="d_ps")
+                for e in range(2):
+                    nc.tensor.matmul(
+                        d_ps[:], lhsT=zbT[:, bt, g, :, e], rhs=dbT[:, cols, e], start=(e == 0), stop=False
+                    )
+                nc.tensor.matmul(d_ps[:], lhsT=ident_bf16[:], rhs=px_sb[:, bt, cols], start=False, stop=True)
+                d_banks.append(d_ps)
+                nc.scalar.copy(out=a_sb[:, cols], in_=a_ps[:])
+                nc.vector.tensor_mul(out=t[:, cols], in0=a_sb[:, cols], in1=w_ps[:])
+            nc.gpsimd.tensor_tensor(out=t[:], in0=t[:], in1=beta[:], op=ALU.add)
+            for half in range(HALVES):
+                cols = slice(half * BANK, (half + 1) * BANK)
+                nc.vector.scalar_tensor_tensor(
+                    out=y[:, cols],
+                    in0=t[:, cols],
+                    scalar=1.0,
+                    in1=d_banks[half][:],
+                    op0=ALU.mult,
+                    op1=ALU.add,
+                    accum_out=ysum[:, half : half + 1],
+                )
+            neg_mu = stats.tile([P, 1], F32, tag="neg_mu")
+            nc.vector.tensor_scalar(
+                out=neg_mu[:], in0=ysum[:, 0:1], scalar1=ysum[:, 1:2], scalar2=-1.0 / H, op0=ALU.add, op1=ALU.mult
+            )
+            sq = work.tile([P, H], F32, tag="sq")
+            ssq = stats.tile([P, 1], F32, tag="ssq")
+            nc.scalar.activation(out=sq[:], in_=y[:], func=ACT.Square, bias=neg_mu[:], scale=1.0, accum_out=ssq[:])
+            var_eps = stats.tile([P, 1], F32, tag="var_eps")
+            nc.gpsimd.tensor_scalar(
+                out=var_eps[:], in0=ssq[:], scalar1=1.0 / H, scalar2=EPS, op0=ALU.mult, op1=ALU.add
+            )
+            rstd = stats.tile([P, 1], F32, tag="rstd")
+            nc.gpsimd.tensor_tensor(out=rstd[:], in0=var_eps[:], in1=neg_half[:], op=ALU.pow)
+            v = work.tile([P, H], F32, tag="v", bufs=3)
+            nc.vector.scalar_tensor_tensor(
+                out=v[:], in0=y[:], scalar=neg_mu[:], in1=lnw[:], op0=ALU.add, op1=ALU.mult
+            )
+            nc.vector.scalar_tensor_tensor(
+                out=v[:], in0=v[:], scalar=rstd[:], in1=lnb[:], op0=ALU.mult, op1=ALU.add
+            )
+            return v
+
+        load_scale_planes(0)
+        batch_raw = [load_batch_tile(0)]
+        gate_in = load_gate(0)
+        for bt in range(1, NBT):
+            batch_raw.append(load_batch_tile(bt))
+
+        for g in range(G):
+            dh_raw, db_raw, words, px_sb, beta, lnw, lnb = gate_in
+            dhT, dbT = prepare_gate(dh_raw, db_raw)
+            if g == 0:
+                nc.sync.dma_start(out=c_sb[:], in_=c.rearrange("(bt p) n -> p bt n", p=P))
+                load_scale_planes(1)
+            if g + 1 < G:
+                gate_in = load_gate(g + 1)
+            for bt in range(NBT):
+                rows = slice(bt * P, (bt + 1) * P)
+                if g == 0:
+                    prepare_batch_tile(bt, *batch_raw[bt])
+                v = gate_preactivation(g, bt, dhT, dbT, words, px_sb, beta, lnw, lnb)
+                if g == 0:
+                    nc.scalar.activation(out=keep_a[:, bt, :], in_=v[:], func=GATE_FUNC[g])
+                elif g == 1:
+                    nc.scalar.activation(out=v[:], in_=v[:], func=GATE_FUNC[g])
+                    nc.vector.tensor_mul(out=keep_b[:, bt, :], in0=v[:], in1=c_sb[:, bt, :])
+                elif g == 2:
+                    nc.scalar.activation(out=v[:], in_=v[:], func=GATE_FUNC[g])
+                    nc.vector.tensor_mul(out=keep_a[:, bt, :], in0=keep_a[:, bt, :], in1=v[:])
+                    nc.vector.tensor_add(out=keep_b[:, bt, :], in0=keep_b[:, bt, :], in1=keep_a[:, bt, :])
+                    nc.sync.dma_start(out=c_next[rows, :], in_=keep_b[:, bt, :])
+                    nc.scalar.activation(out=keep_a[:, bt, :], in_=keep_b[:, bt, :], func=ACT.Tanh)
+                else:
+                    nc.scalar.activation(out=v[:], in_=v[:], func=GATE_FUNC[g])
+                    nc.vector.tensor_mul(out=v[:], in0=v[:], in1=keep_a[:, bt, :])
+                    nc.sync.dma_start(out=h_next[rows, :], in_=v[:])

@@ -16,6 +16,7 @@ P = 128
 B, H, Z, G = 512, 1024, 256, 4
 EPS = 1e-5
 NBT = B // P
+UNITS = G * NBT
 BANK = 512
 HALVES = H // BANK
 K_PASS = 512
@@ -32,9 +33,11 @@ def tile_metalstmcell_pb_e_kernel(
 ):
     nc = tc.nc
     with ExitStack() as ctx:
+        ctx.enter_context(tc.manual_schedule())
         const = ctx.enter_context(tc.tile_pool(name="const", bufs=1))
         raw = ctx.enter_context(tc.tile_pool(name="raw", bufs=NBT))
         gatew = ctx.enter_context(tc.tile_pool(name="gatew", bufs=2))
+        rows_pool = ctx.enter_context(tc.tile_pool(name="rows", bufs=3))
         work = ctx.enter_context(tc.tile_pool(name="work", bufs=2))
         stats = ctx.enter_context(tc.tile_pool(name="stats", bufs=4))
         psum_t = ctx.enter_context(tc.psum_pool(name="psum_t", bufs=2))
@@ -57,6 +60,16 @@ def tile_metalstmcell_pb_e_kernel(
         keep_a = const.tile([P, NBT, H], F32)
         keep_b = const.tile([P, NBT, H], F32)
 
+        batch_raw = {}
+        gate_raw = {}
+        gate_mx = {}
+        gate_px = {}
+        gate_rows = {}
+        gate_T = {}
+        neg_beta_mean = {}
+        banks = {}
+        a_sbs, ys, neg_mus, ssqs, rstds, vs = {}, {}, {}, {}, {}, {}
+
         def load_scale_planes(j):
             for q in range(4):
                 nc.sync.dma_start(
@@ -72,13 +85,14 @@ def tile_metalstmcell_pb_e_kernel(
             nc.sync.dma_start(out=zh_raw[:], in_=zh[rows])
             zb_raw = raw.tile([P, G, Z], BF16, tag="zb_raw")
             nc.sync.dma_start(out=zb_raw[:], in_=zb[rows])
-            return h_raw, zh_raw, zb_raw
+            batch_raw[bt] = (h_raw, zh_raw, zb_raw)
 
-        def load_gate(g):
+        def load_gate_matrices(g):
             dh_raw = gatew.tile([P, H // P, Z], BF16, tag="dh_raw")
             nc.sync.dma_start(out=dh_raw[:], in_=dh_w[g].rearrange("(nt p) z -> p nt z", p=P))
             db_raw = gatew.tile([P, H // P, Z], BF16, tag="db_raw")
             nc.sync.dma_start(out=db_raw[:], in_=db_w[g].rearrange("(nt p) z -> p nt z", p=P))
+            gate_raw[g] = (dh_raw, db_raw)
             words = gatew.tile([P, PASSES, H], U32, tag="words", align_bytes=64)
             nc.sync.dma_start(
                 out=words[:].bitcast(I32),
@@ -86,15 +100,25 @@ def tile_metalstmcell_pb_e_kernel(
                 .rearrange("s p n t -> p s (n t)")
                 .bitcast(I32),
             )
+            gate_mx[g] = words
             px_sb = gatew.tile([P, NBT, H], BF16, tag="px_sb")
-            nc.sync.dma_start(out=px_sb[:], in_=px[:, g, :].rearrange("(bt p) n -> p bt n", p=P))
-            beta = gatew.tile([P, H], BF16, tag="beta")
-            nc.sync.dma_start(out=beta[:], in_=db_b[g].partition_broadcast(P))
-            lnw = gatew.tile([P, H], BF16, tag="lnw")
-            nc.sync.dma_start(out=lnw[:], in_=ln_w[g].partition_broadcast(P))
-            lnb = gatew.tile([P, H], BF16, tag="lnb")
-            nc.sync.dma_start(out=lnb[:], in_=ln_b[g].partition_broadcast(P))
-            return dh_raw, db_raw, words, px_sb, beta, lnw, lnb
+            gate_px[g] = px_sb
+
+        def load_px(g, bt):
+            nc.sync.dma_start(out=gate_px[g][:, bt, :], in_=px[bt * P : (bt + 1) * P, g, :])
+
+        def load_row(name, vector, g):
+            row = rows_pool.tile([P, H], BF16, tag=name)
+            nc.sync.dma_start(out=row[:], in_=vector[g].partition_broadcast(P))
+            gate_rows[(name, g)] = row
+
+        def load_gate(g):
+            load_gate_matrices(g)
+            for bt in range(NBT):
+                load_px(g, bt)
+            load_row("beta", db_b, g)
+            load_row("lnw", ln_w, g)
+            load_row("lnb", ln_b, g)
 
         def transpose_pairs(word_blocks, dst):
             tp = psum_t.tile([P, 4, P], F32, tag="tp")
@@ -102,7 +126,8 @@ def tile_metalstmcell_pb_e_kernel(
                 nc.tensor.transpose(tp[:, j, :], word_blocks[:, j, :], ident_f32[:])
             nc.scalar.copy(out=dst, in_=tp[:].bitcast(BF16))
 
-        def prepare_batch_tile(bt, h_raw, zh_raw, zb_raw):
+        def prepare_batch_tile(bt):
+            h_raw, zh_raw, zb_raw = batch_raw[bt]
             transpose_pairs(zh_raw[:].bitcast(F32), zhT[:, bt].rearrange("p g b e -> p g (b e)"))
             transpose_pairs(zb_raw[:].bitcast(F32), zbT[:, bt].rearrange("p g b e -> p g (b e)"))
             h_words = h_raw[:].bitcast(F32)
@@ -124,29 +149,44 @@ def tile_metalstmcell_pb_e_kernel(
                 in_=grouped[:].rearrange("p s b t -> p (s b t)"),
             )
 
-        def prepare_gate(dh_raw, db_raw):
-            dhT = gatew.tile([P, H, 2], BF16, tag="dhT")
-            dbT = gatew.tile([P, H, 2], BF16, tag="dbT")
-            for src, dst in ((dh_raw, dhT), (db_raw, dbT)):
-                src_words = src[:].bitcast(F32)
-                dst_blocks = dst[:].rearrange("p (nt r) e -> p nt (r e)", r=P)
-                for q in range(H // P // 4):
-                    transpose_pairs(src_words[:, 4 * q : 4 * q + 4, :], dst_blocks[:, 4 * q : 4 * q + 4, :])
-            return dhT, dbT
+        def prepare_gate_matrix(name, g):
+            src = gate_raw[g][0 if name == "dhT" else 1]
+            dst = gatew.tile([P, H, 2], BF16, tag=name)
+            src_words = src[:].bitcast(F32)
+            dst_blocks = dst[:].rearrange("p (nt r) e -> p nt (r e)", r=P)
+            for q in range(H // P // 4):
+                transpose_pairs(src_words[:, 4 * q : 4 * q + 4, :], dst_blocks[:, 4 * q : 4 * q + 4, :])
+            gate_T[(name, g)] = dst
 
-        def gate_preactivation(g, bt, dhT, dbT, words, px_sb, beta, lnw, lnb):
+        def prepare_beta_mean(g):
+            junk = work.tile([P, H], F32, tag="sq")
+            nbm = stats.tile([P, 1], F32, tag="nbm")
+            nc.scalar.activation(
+                out=junk[:], in_=gate_rows[("beta", g)][:], func=ACT.Copy, scale=-1.0 / H, accum_out=nbm[:]
+            )
+            neg_beta_mean[g] = nbm
+
+        def scale_matmuls(k):
+            g, bt = divmod(k, NBT)
             a_sb = work.tile([P, H], F32, tag="a_sb")
-            t = work.tile([P, H], F32, tag="t")
-            y = work.tile([P, H], F32, tag="y", bufs=3)
-            ysum = stats.tile([P, HALVES], F32, tag="ysum")
-            d_banks = []
             for half in range(HALVES):
                 cols = slice(half * BANK, (half + 1) * BANK)
                 a_ps = psum_m.tile([P, BANK], F32, tag="a_ps")
                 for e in range(2):
                     nc.tensor.matmul(
-                        a_ps[:], lhsT=zhT[:, bt, g, :, e], rhs=dhT[:, cols, e], start=(e == 0), stop=(e == 1)
+                        a_ps[:],
+                        lhsT=zhT[:, bt, g, :, e],
+                        rhs=gate_T[("dhT", g)][:, cols, e],
+                        start=(e == 0),
+                        stop=(e == 1),
                     )
+                nc.scalar.copy(out=a_sb[:, cols], in_=a_ps[:])
+            a_sbs[k] = a_sb
+
+        def other_matmuls(k):
+            g, bt = divmod(k, NBT)
+            for half in range(HALVES):
+                cols = slice(half * BANK, (half + 1) * BANK)
                 w_ps = psum_m.tile([P, BANK], F32, tag="w_ps")
                 for s in range(PASSES):
                     group = PASSES * g + s
@@ -155,85 +195,161 @@ def tile_metalstmcell_pb_e_kernel(
                         out=w_ps[:],
                         lhsT=h_codes[:, bt, s * P : (s + 1) * P].bitcast(FP8X4),
                         lhsT_scale=h_scales[:, bt, s * P : (s + 1) * P],
-                        rhs=words[:, s, cols].bitcast(FP8X4),
+                        rhs=gate_mx[g][:, s, cols].bitcast(FP8X4),
                         rhs_scale=planes[row0:P, group // PLANES, cols],
                         start=(s == 0),
                         stop=(s == PASSES - 1),
                     )
+                banks[("w", k, half)] = w_ps
+            for half in range(HALVES):
+                cols = slice(half * BANK, (half + 1) * BANK)
                 d_ps = psum_m.tile([P, BANK], F32, tag="d_ps")
                 for e in range(2):
                     nc.tensor.matmul(
-                        d_ps[:], lhsT=zbT[:, bt, g, :, e], rhs=dbT[:, cols, e], start=(e == 0), stop=False
+                        d_ps[:],
+                        lhsT=zbT[:, bt, g, :, e],
+                        rhs=gate_T[("dbT", g)][:, cols, e],
+                        start=(e == 0),
+                        stop=False,
                     )
-                nc.tensor.matmul(d_ps[:], lhsT=ident_bf16[:], rhs=px_sb[:, bt, cols], start=False, stop=True)
-                d_banks.append(d_ps)
-                nc.scalar.copy(out=a_sb[:, cols], in_=a_ps[:])
-                nc.vector.tensor_mul(out=t[:, cols], in0=a_sb[:, cols], in1=w_ps[:])
-            nc.gpsimd.tensor_tensor(out=t[:], in0=t[:], in1=beta[:], op=ALU.add)
+                nc.tensor.matmul(
+                    d_ps[:], lhsT=ident_bf16[:], rhs=gate_px[g][:, bt, cols], start=False, stop=True
+                )
+                banks[("d", k, half)] = d_ps
+
+        def products(k):
+            g = k // NBT
+            t = work.tile([P, H], F32, tag="t")
+            y = work.tile([P, H], F32, tag="y")
+            ysum = stats.tile([P, HALVES], F32, tag="ysum")
+            for half in range(HALVES):
+                cols = slice(half * BANK, (half + 1) * BANK)
+                nc.vector.tensor_mul(out=t[:, cols], in0=a_sbs[k][:, cols], in1=banks[("w", k, half)][:])
             for half in range(HALVES):
                 cols = slice(half * BANK, (half + 1) * BANK)
                 nc.vector.scalar_tensor_tensor(
                     out=y[:, cols],
                     in0=t[:, cols],
                     scalar=1.0,
-                    in1=d_banks[half][:],
+                    in1=banks[("d", k, half)][:],
                     op0=ALU.mult,
                     op1=ALU.add,
                     accum_out=ysum[:, half : half + 1],
                 )
-            neg_mu = stats.tile([P, 1], F32, tag="neg_mu")
+            neg_mu0 = stats.tile([P, 1], F32, tag="neg_mu0")
             nc.vector.tensor_scalar(
-                out=neg_mu[:], in0=ysum[:, 0:1], scalar1=ysum[:, 1:2], scalar2=-1.0 / H, op0=ALU.add, op1=ALU.mult
+                out=neg_mu0[:], in0=ysum[:, 0:1], scalar1=ysum[:, 1:2], scalar2=-1.0 / H, op0=ALU.add, op1=ALU.mult
             )
+            neg_mu = stats.tile([P, 1], F32, tag="neg_mu")
+            nc.vector.tensor_add(out=neg_mu[:], in0=neg_mu0[:], in1=neg_beta_mean[g][:])
+            ys[k] = y
+            neg_mus[k] = neg_mu
+
+        def add_bias(k):
+            nc.gpsimd.tensor_tensor(out=ys[k][:], in0=ys[k][:], in1=gate_rows[("beta", k // NBT)][:], op=ALU.add)
+
+        def squares(k):
             sq = work.tile([P, H], F32, tag="sq")
             ssq = stats.tile([P, 1], F32, tag="ssq")
-            nc.scalar.activation(out=sq[:], in_=y[:], func=ACT.Square, bias=neg_mu[:], scale=1.0, accum_out=ssq[:])
+            nc.scalar.activation(
+                out=sq[:], in_=ys[k][:], func=ACT.Square, bias=neg_mus[k][:], scale=1.0, accum_out=ssq[:]
+            )
+            ssqs[k] = ssq
+
+        def inverse_std(k):
             var_eps = stats.tile([P, 1], F32, tag="var_eps")
             nc.gpsimd.tensor_scalar(
-                out=var_eps[:], in0=ssq[:], scalar1=1.0 / H, scalar2=EPS, op0=ALU.mult, op1=ALU.add
+                out=var_eps[:], in0=ssqs[k][:], scalar1=1.0 / H, scalar2=EPS, op0=ALU.mult, op1=ALU.add
             )
             rstd = stats.tile([P, 1], F32, tag="rstd")
             nc.gpsimd.tensor_tensor(out=rstd[:], in0=var_eps[:], in1=neg_half[:], op=ALU.pow)
+            rstds[k] = rstd
+
+        def centre_and_gain(k):
             v = work.tile([P, H], F32, tag="v", bufs=3)
             nc.vector.scalar_tensor_tensor(
-                out=v[:], in0=y[:], scalar=neg_mu[:], in1=lnw[:], op0=ALU.add, op1=ALU.mult
+                out=v[:], in0=ys[k][:], scalar=neg_mus[k][:], in1=gate_rows[("lnw", k // NBT)][:],
+                op0=ALU.add, op1=ALU.mult,
             )
+            vs[k] = v
+
+        def scale_and_shift(k):
             nc.vector.scalar_tensor_tensor(
-                out=v[:], in0=v[:], scalar=rstd[:], in1=lnb[:], op0=ALU.mult, op1=ALU.add
+                out=vs[k][:], in0=vs[k][:], scalar=rstds[k][:], in1=gate_rows[("lnb", k // NBT)][:],
+                op0=ALU.mult, op1=ALU.add,
             )
-            return v
+
+        def activate(k):
+            g, bt = divmod(k, NBT)
+            dst = keep_a[:, bt, :] if g == 0 else vs[k][:]
+            nc.scalar.activation(out=dst, in_=vs[k][:], func=GATE_FUNC[g])
+
+        def cell(k):
+            g, bt = divmod(k, NBT)
+            rows = slice(bt * P, (bt + 1) * P)
+            if g == 1:
+                nc.vector.tensor_mul(out=keep_b[:, bt, :], in0=vs[k][:], in1=c_sb[:, bt, :])
+            elif g == 2:
+                nc.vector.tensor_mul(out=keep_a[:, bt, :], in0=keep_a[:, bt, :], in1=vs[k][:])
+                nc.vector.tensor_add(out=keep_b[:, bt, :], in0=keep_b[:, bt, :], in1=keep_a[:, bt, :])
+                nc.sync.dma_start(out=c_next[rows, :], in_=keep_b[:, bt, :])
+                nc.scalar.activation(out=keep_a[:, bt, :], in_=keep_b[:, bt, :], func=ACT.Tanh)
+            elif g == 3:
+                nc.vector.tensor_mul(out=vs[k][:], in0=vs[k][:], in1=keep_a[:, bt, :])
+                nc.sync.dma_start(out=h_next[rows, :], in_=vs[k][:])
 
         load_scale_planes(0)
-        batch_raw = [load_batch_tile(0)]
-        gate_in = load_gate(0)
-        for bt in range(1, NBT):
-            batch_raw.append(load_batch_tile(bt))
+        load_batch_tile(0)
+        load_gate_matrices(0)
+        load_px(0, 0)
+        load_row("beta", db_b, 0)
+        load_batch_tile(1)
+        load_px(0, 1)
+        load_row("lnw", ln_w, 0)
+        load_row("lnb", ln_b, 0)
+        for bt in range(2, NBT):
+            load_batch_tile(bt)
+            load_px(0, bt)
+        nc.sync.dma_start(out=c_sb[:], in_=c.rearrange("(bt p) n -> p bt n", p=P))
+        load_scale_planes(1)
+        load_gate(1)
 
-        for g in range(G):
-            dh_raw, db_raw, words, px_sb, beta, lnw, lnb = gate_in
-            dhT, dbT = prepare_gate(dh_raw, db_raw)
-            if g == 0:
-                nc.sync.dma_start(out=c_sb[:], in_=c.rearrange("(bt p) n -> p bt n", p=P))
-                load_scale_planes(1)
-            if g + 1 < G:
-                gate_in = load_gate(g + 1)
-            for bt in range(NBT):
-                rows = slice(bt * P, (bt + 1) * P)
-                if g == 0:
-                    prepare_batch_tile(bt, *batch_raw[bt])
-                v = gate_preactivation(g, bt, dhT, dbT, words, px_sb, beta, lnw, lnb)
-                if g == 0:
-                    nc.scalar.activation(out=keep_a[:, bt, :], in_=v[:], func=GATE_FUNC[g])
-                elif g == 1:
-                    nc.scalar.activation(out=v[:], in_=v[:], func=GATE_FUNC[g])
-                    nc.vector.tensor_mul(out=keep_b[:, bt, :], in0=v[:], in1=c_sb[:, bt, :])
-                elif g == 2:
-                    nc.scalar.activation(out=v[:], in_=v[:], func=GATE_FUNC[g])
-                    nc.vector.tensor_mul(out=keep_a[:, bt, :], in0=keep_a[:, bt, :], in1=v[:])
-                    nc.vector.tensor_add(out=keep_b[:, bt, :], in0=keep_b[:, bt, :], in1=keep_a[:, bt, :])
-                    nc.sync.dma_start(out=c_next[rows, :], in_=keep_b[:, bt, :])
-                    nc.scalar.activation(out=keep_a[:, bt, :], in_=keep_b[:, bt, :], func=ACT.Tanh)
-                else:
-                    nc.scalar.activation(out=v[:], in_=v[:], func=GATE_FUNC[g])
-                    nc.vector.tensor_mul(out=v[:], in0=v[:], in1=keep_a[:, bt, :])
-                    nc.sync.dma_start(out=h_next[rows, :], in_=v[:])
+        prepare_batch_tile(0)
+        prepare_gate_matrix("dhT", 0)
+        prepare_gate_matrix("dbT", 0)
+        scale_matmuls(0)
+        other_matmuls(0)
+        prepare_batch_tile(1)
+        prepare_beta_mean(0)
+
+        for step in range(UNITS + 3):
+            g, bt = divmod(step, NBT)
+            if step + 1 < UNITS:
+                scale_matmuls(step + 1)
+            if step < UNITS:
+                products(step)
+            if step + 1 < UNITS:
+                other_matmuls(step + 1)
+            if 0 <= step - 1 < UNITS:
+                add_bias(step - 1)
+            if 0 <= step - 2 < UNITS:
+                inverse_std(step - 2)
+            if step + 2 < NBT:
+                prepare_batch_tile(step + 2)
+            if 1 <= g and g + 1 < G and bt == 0:
+                load_gate(g + 1)
+            if g + 1 < G and bt == 1:
+                prepare_gate_matrix("dhT", g + 1)
+            if g + 1 < G and bt == 2:
+                prepare_gate_matrix("dbT", g + 1)
+                prepare_beta_mean(g + 1)
+            if 0 <= step - 1 < UNITS:
+                squares(step - 1)
+            if 0 <= step - 1 < UNITS:
+                centre_and_gain(step - 1)
+            if 0 <= step - 2 < UNITS:
+                scale_and_shift(step - 2)
+            if 0 <= step - 2 < UNITS:
+                activate(step - 2)
+            if 0 <= step - 3 < UNITS:
+                cell(step - 3)

@@ -22,6 +22,8 @@ HALVES = H // BANK
 K_PASS = 512
 PASSES = H // K_PASS
 PLANES = 4
+QUARTERS = 4
+ROW_INDEX = {"beta": 0, "lnw": 1, "lnb": 2}
 
 FLOPS = 2 * B * G * H * (H + 2 * Z)
 
@@ -37,11 +39,10 @@ def tile_metalstmcell_pb_e_kernel(
         const = ctx.enter_context(tc.tile_pool(name="const", bufs=1))
         raw = ctx.enter_context(tc.tile_pool(name="raw", bufs=NBT))
         gatew = ctx.enter_context(tc.tile_pool(name="gatew", bufs=2))
-        rows_pool = ctx.enter_context(tc.tile_pool(name="rows", bufs=3))
         work = ctx.enter_context(tc.tile_pool(name="work", bufs=2))
         stats = ctx.enter_context(tc.tile_pool(name="stats", bufs=4))
-        psum_t = ctx.enter_context(tc.psum_pool(name="psum_t", bufs=2))
         psum_m = ctx.enter_context(tc.psum_pool(name="psum_m", bufs=2))
+        psum_ln = ctx.enter_context(tc.psum_pool(name="psum_ln", bufs=1))
 
         planes = const.tile([P, 8 // PLANES, H], U8, align_bytes=64)
         nc.vector.memset(planes[:].bitcast(I32), 0)
@@ -51,6 +52,10 @@ def tile_metalstmcell_pb_e_kernel(
         make_identity(nc, ident_bf16[:])
         neg_half = const.tile([P, 1], F32)
         nc.gpsimd.memset(neg_half[:], -0.5)
+
+        rows_raw = const.tile([P, 2 * P], BF16)
+        nc.vector.memset(rows_raw[:], 0.0)
+        rowsT = const.tile([P, 2 * P], BF16)
 
         h_codes = const.tile([P, NBT, PASSES * P], U32, align_bytes=64)
         h_scales = const.tile([P, NBT, PASSES * P], U8, align_bytes=64)
@@ -68,7 +73,7 @@ def tile_metalstmcell_pb_e_kernel(
         gate_T = {}
         neg_beta_mean = {}
         banks = {}
-        a_sbs, ys, neg_mus, ssqs, rstds, vs = {}, {}, {}, {}, {}, {}
+        a_sbs, ys, ysums, neg_mus, ssqs, rstds, vs = {}, {}, {}, {}, {}, {}, {}
 
         def load_scale_planes(j):
             for q in range(4):
@@ -107,31 +112,60 @@ def tile_metalstmcell_pb_e_kernel(
         def load_px(g, bt):
             nc.sync.dma_start(out=gate_px[g][:, bt, :], in_=px[bt * P : (bt + 1) * P, g, :])
 
-        def load_row(name, vector, g):
-            row = rows_pool.tile([P, H], BF16, tag=name)
-            nc.sync.dma_start(out=row[:], in_=vector[g].partition_broadcast(P))
-            gate_rows[(name, g)] = row
+        def load_rows():
+            for i, vector in enumerate((db_b, ln_w, ln_b)):
+                nc.sync.dma_start(
+                    out=rows_raw[G * QUARTERS * i : G * QUARTERS * (i + 1), :],
+                    in_=vector.rearrange("g (q w) -> (g q) w", q=QUARTERS),
+                )
 
         def load_gate(g):
             load_gate_matrices(g)
             for bt in range(NBT):
                 load_px(g, bt)
-            load_row("beta", db_b, g)
-            load_row("lnw", ln_w, g)
-            load_row("lnb", ln_b, g)
 
         def transpose_pairs(word_blocks, dst):
-            tp = psum_t.tile([P, 4, P], F32, tag="tp")
+            tp = psum_m.tile([P, 4, P], F32, tag="a_ps")
             for j in range(4):
                 nc.tensor.transpose(tp[:, j, :], word_blocks[:, j, :], ident_f32[:])
             nc.scalar.copy(out=dst, in_=tp[:].bitcast(BF16))
+
+        def prepare_rows():
+            tp = psum_m.tile([P, 4, P], F32, tag="a_ps")
+            nc.tensor.transpose(tp[:, 0, :], rows_raw[:].bitcast(F32), ident_f32[:])
+            nc.scalar.copy(out=rowsT[:], in_=tp[:, 0, :].bitcast(BF16))
+
+        def spread_row(name, g, bank):
+            for q in range(QUARTERS):
+                r = G * QUARTERS * ROW_INDEX[name] + QUARTERS * g + q
+                nc.tensor.transpose(
+                    bank[:, q * P : (q + 1) * P],
+                    rowsT[:].bitcast(F32)[:, r : r + 1].to_broadcast([P, P]),
+                    ident_f32[:],
+                )
+
+        def spread_ln_row(name, g):
+            bank = psum_ln.tile([P, BANK], F32, tag=name)
+            spread_row(name, g, bank)
+            gate_rows[(name, g)] = bank[:].bitcast(BF16)
+
+        def spread_beta(g):
+            bank = psum_m.tile([P, BANK], F32, tag="a_ps")
+            spread_row("beta", g, bank)
+            beta = gatew.tile([P, H], BF16, tag="beta")
+            nc.scalar.copy(out=beta[:], in_=bank[:].bitcast(BF16))
+            gate_rows[("beta", g)] = beta[:]
+            junk = work.tile([P, H], F32, tag="sq")
+            nbm = stats.tile([P, 1], F32, tag="nbm")
+            nc.scalar.activation(out=junk[:], in_=beta[:], func=ACT.Copy, scale=-0.5 / H, accum_out=nbm[:])
+            neg_beta_mean[g] = nbm
 
         def prepare_batch_tile(bt):
             h_raw, zh_raw, zb_raw = batch_raw[bt]
             transpose_pairs(zh_raw[:].bitcast(F32), zhT[:, bt].rearrange("p g b e -> p g (b e)"))
             transpose_pairs(zb_raw[:].bitcast(F32), zbT[:, bt].rearrange("p g b e -> p g (b e)"))
             h_words = h_raw[:].bitcast(F32)
-            tp = psum_t.tile([P, 4, P], F32, tag="tp")
+            tp = psum_m.tile([P, 4, P], F32, tag="a_ps")
             for s in range(PASSES):
                 for u in range(2):
                     nc.tensor.transpose(
@@ -157,14 +191,6 @@ def tile_metalstmcell_pb_e_kernel(
             for q in range(H // P // 4):
                 transpose_pairs(src_words[:, 4 * q : 4 * q + 4, :], dst_blocks[:, 4 * q : 4 * q + 4, :])
             gate_T[(name, g)] = dst
-
-        def prepare_beta_mean(g):
-            junk = work.tile([P, H], F32, tag="sq")
-            nbm = stats.tile([P, 1], F32, tag="nbm")
-            nc.scalar.activation(
-                out=junk[:], in_=gate_rows[("beta", g)][:], func=ACT.Copy, scale=-1.0 / H, accum_out=nbm[:]
-            )
-            neg_beta_mean[g] = nbm
 
         def scale_matmuls(k):
             g, bt = divmod(k, NBT)
@@ -218,7 +244,6 @@ def tile_metalstmcell_pb_e_kernel(
                 banks[("d", k, half)] = d_ps
 
         def products(k):
-            g = k // NBT
             t = work.tile([P, H], F32, tag="t")
             y = work.tile([P, H], F32, tag="y")
             ysum = stats.tile([P, HALVES], F32, tag="ysum")
@@ -236,17 +261,20 @@ def tile_metalstmcell_pb_e_kernel(
                     op1=ALU.add,
                     accum_out=ysum[:, half : half + 1],
                 )
-            neg_mu0 = stats.tile([P, 1], F32, tag="neg_mu0")
-            nc.vector.tensor_scalar(
-                out=neg_mu0[:], in0=ysum[:, 0:1], scalar1=ysum[:, 1:2], scalar2=-1.0 / H, op0=ALU.add, op1=ALU.mult
-            )
-            neg_mu = stats.tile([P, 1], F32, tag="neg_mu")
-            nc.vector.tensor_add(out=neg_mu[:], in0=neg_mu0[:], in1=neg_beta_mean[g][:])
             ys[k] = y
+            ysums[k] = ysum
+
+        def mean(k):
+            junk2 = stats.tile([P, HALVES], F32, tag="junk2")
+            neg_mu = stats.tile([P, 1], F32, tag="neg_mu")
+            nc.scalar.activation(
+                out=junk2[:], in_=ysums[k][:], func=ACT.Identity, scale=-1.0 / H,
+                bias=neg_beta_mean[k // NBT][:], accum_out=neg_mu[:],
+            )
             neg_mus[k] = neg_mu
 
         def add_bias(k):
-            nc.gpsimd.tensor_tensor(out=ys[k][:], in0=ys[k][:], in1=gate_rows[("beta", k // NBT)][:], op=ALU.add)
+            nc.gpsimd.tensor_tensor(out=ys[k][:], in0=ys[k][:], in1=gate_rows[("beta", k // NBT)], op=ALU.add)
 
         def squares(k):
             sq = work.tile([P, H], F32, tag="sq")
@@ -268,14 +296,14 @@ def tile_metalstmcell_pb_e_kernel(
         def centre_and_gain(k):
             v = work.tile([P, H], F32, tag="v", bufs=3)
             nc.vector.scalar_tensor_tensor(
-                out=v[:], in0=ys[k][:], scalar=neg_mus[k][:], in1=gate_rows[("lnw", k // NBT)][:],
+                out=v[:], in0=ys[k][:], scalar=neg_mus[k][:], in1=gate_rows[("lnw", k // NBT)],
                 op0=ALU.add, op1=ALU.mult,
             )
             vs[k] = v
 
         def scale_and_shift(k):
             nc.vector.scalar_tensor_tensor(
-                out=vs[k][:], in0=vs[k][:], scalar=rstds[k][:], in1=gate_rows[("lnb", k // NBT)][:],
+                out=vs[k][:], in0=vs[k][:], scalar=rstds[k][:], in1=gate_rows[("lnb", k // NBT)],
                 op0=ALU.mult, op1=ALU.add,
             )
 
@@ -284,56 +312,71 @@ def tile_metalstmcell_pb_e_kernel(
             dst = keep_a[:, bt, :] if g == 0 else vs[k][:]
             nc.scalar.activation(out=dst, in_=vs[k][:], func=GATE_FUNC[g])
 
-        def cell(k):
+        def cell_on_gpsimd(k):
             g, bt = divmod(k, NBT)
-            rows = slice(bt * P, (bt + 1) * P)
             if g == 1:
-                nc.vector.tensor_mul(out=keep_b[:, bt, :], in0=vs[k][:], in1=c_sb[:, bt, :])
-            elif g == 2:
+                nc.gpsimd.tensor_tensor(out=keep_b[:, bt, :], in0=vs[k][:], in1=c_sb[:, bt, :], op=ALU.mult)
+            elif g == 3:
+                nc.gpsimd.tensor_tensor(out=vs[k][:], in0=vs[k][:], in1=keep_a[:, bt, :], op=ALU.mult)
+                nc.sync.dma_start(out=h_next[bt * P : (bt + 1) * P, :], in_=vs[k][:])
+
+        def cell_on_vector(k):
+            g, bt = divmod(k, NBT)
+            if g == 2:
                 nc.vector.tensor_mul(out=keep_a[:, bt, :], in0=keep_a[:, bt, :], in1=vs[k][:])
                 nc.vector.tensor_add(out=keep_b[:, bt, :], in0=keep_b[:, bt, :], in1=keep_a[:, bt, :])
-                nc.sync.dma_start(out=c_next[rows, :], in_=keep_b[:, bt, :])
+                nc.sync.dma_start(out=c_next[bt * P : (bt + 1) * P, :], in_=keep_b[:, bt, :])
                 nc.scalar.activation(out=keep_a[:, bt, :], in_=keep_b[:, bt, :], func=ACT.Tanh)
-            elif g == 3:
-                nc.vector.tensor_mul(out=vs[k][:], in0=vs[k][:], in1=keep_a[:, bt, :])
-                nc.sync.dma_start(out=h_next[rows, :], in_=vs[k][:])
 
+        load_rows()
         load_scale_planes(0)
         load_batch_tile(0)
         load_gate_matrices(0)
         load_px(0, 0)
-        load_row("beta", db_b, 0)
-        load_batch_tile(1)
-        load_px(0, 1)
-        load_row("lnw", ln_w, 0)
-        load_row("lnb", ln_b, 0)
-        for bt in range(2, NBT):
+        for bt in range(1, NBT):
             load_batch_tile(bt)
             load_px(0, bt)
         nc.sync.dma_start(out=c_sb[:], in_=c.rearrange("(bt p) n -> p bt n", p=P))
         load_scale_planes(1)
         load_gate(1)
 
+        prepare_rows()
         prepare_batch_tile(0)
         prepare_gate_matrix("dhT", 0)
         prepare_gate_matrix("dbT", 0)
         scale_matmuls(0)
         other_matmuls(0)
+        spread_beta(0)
+        spread_ln_row("lnw", 0)
+        spread_ln_row("lnb", 0)
         prepare_batch_tile(1)
-        prepare_beta_mean(0)
 
         for step in range(UNITS + 3):
             g, bt = divmod(step, NBT)
+            if 0 <= step - 1 < UNITS:
+                squares(step - 1)
             if step + 1 < UNITS:
                 scale_matmuls(step + 1)
             if step < UNITS:
                 products(step)
             if step + 1 < UNITS:
                 other_matmuls(step + 1)
+            if step < UNITS:
+                mean(step)
+            if 0 <= step - 3 < UNITS:
+                cell_on_gpsimd(step - 3)
             if 0 <= step - 1 < UNITS:
-                add_bias(step - 1)
+                inverse_std(step - 1)
+            if step < UNITS:
+                add_bias(step)
             if 0 <= step - 2 < UNITS:
-                inverse_std(step - 2)
+                scale_and_shift(step - 2)
+            if 0 <= step - 1 < UNITS:
+                centre_and_gain(step - 1)
+            if 0 <= step - 2 < UNITS:
+                activate(step - 2)
+            if 0 <= step - 3 < UNITS:
+                cell_on_vector(step - 3)
             if step + 2 < NBT:
                 prepare_batch_tile(step + 2)
             if 1 <= g and g + 1 < G and bt == 0:
@@ -342,14 +385,8 @@ def tile_metalstmcell_pb_e_kernel(
                 prepare_gate_matrix("dhT", g + 1)
             if g + 1 < G and bt == 2:
                 prepare_gate_matrix("dbT", g + 1)
-                prepare_beta_mean(g + 1)
-            if 0 <= step - 1 < UNITS:
-                squares(step - 1)
-            if 0 <= step - 1 < UNITS:
-                centre_and_gain(step - 1)
-            if 0 <= step - 2 < UNITS:
-                scale_and_shift(step - 2)
-            if 0 <= step - 2 < UNITS:
-                activate(step - 2)
-            if 0 <= step - 3 < UNITS:
-                cell(step - 3)
+                spread_beta(g + 1)
+            if 1 <= g < G and bt == 0:
+                spread_ln_row("lnw", g)
+            if 1 <= g < G and bt == 1:
+                spread_ln_row("lnb", g)

@@ -23,7 +23,7 @@ K_PASS = 512
 PASSES = H // K_PASS
 PLANES = 4
 QUARTERS = 4
-ROW_INDEX = {"beta": 0, "lnw": 1, "lnb": 2}
+ROW_INDEX = {"lnw": 0, "lnb": 1}
 
 FLOPS = 2 * B * G * H * (H + 2 * Z)
 
@@ -52,10 +52,15 @@ def tile_metalstmcell_pb_e_kernel(
         make_identity(nc, ident_bf16[:])
         neg_half = const.tile([P, 1], F32)
         nc.gpsimd.memset(neg_half[:], -0.5)
+        eps_col = const.tile([P, 1], F32)
+        nc.gpsimd.memset(eps_col[:], EPS)
 
         rows_raw = const.tile([P, 2 * P], BF16)
         nc.vector.memset(rows_raw[:], 0.0)
         rowsT = const.tile([P, 2 * P], BF16)
+        beta_raw = const.tile([P, P], BF16)
+        nc.vector.memset(beta_raw[:], 0.0)
+        betaT = const.tile([P, P], F32)
 
         h_codes = const.tile([P, NBT, PASSES * P], U32, align_bytes=64)
         h_scales = const.tile([P, NBT, PASSES * P], U8, align_bytes=64)
@@ -71,7 +76,6 @@ def tile_metalstmcell_pb_e_kernel(
         gate_px = {}
         gate_rows = {}
         gate_T = {}
-        neg_beta_mean = {}
         banks = {}
         a_sbs, ys, ysums, neg_mus, ssqs, rstds, vs = {}, {}, {}, {}, {}, {}, {}
 
@@ -98,6 +102,8 @@ def tile_metalstmcell_pb_e_kernel(
             db_raw = gatew.tile([P, H // P, Z], BF16, tag="db_raw")
             nc.sync.dma_start(out=db_raw[:], in_=db_w[g].rearrange("(nt p) z -> p nt z", p=P))
             gate_raw[g] = (dh_raw, db_raw)
+
+        def load_gate_words(g):
             words = gatew.tile([P, PASSES, H], U32, tag="words", align_bytes=64)
             nc.sync.dma_start(
                 out=words[:].bitcast(I32),
@@ -113,14 +119,16 @@ def tile_metalstmcell_pb_e_kernel(
             nc.sync.dma_start(out=gate_px[g][:, bt, :], in_=px[bt * P : (bt + 1) * P, g, :])
 
         def load_rows():
-            for i, vector in enumerate((db_b, ln_w, ln_b)):
+            for i, vector in enumerate((ln_w, ln_b)):
                 nc.sync.dma_start(
                     out=rows_raw[G * QUARTERS * i : G * QUARTERS * (i + 1), :],
                     in_=vector.rearrange("g (q w) -> (g q) w", q=QUARTERS),
                 )
+            nc.sync.dma_start(out=beta_raw[0 : G * (H // P), :], in_=db_b.rearrange("g (j w) -> (g j) w", w=P))
 
         def load_gate(g):
             load_gate_matrices(g)
+            load_gate_words(g)
             for bt in range(NBT):
                 load_px(g, bt)
 
@@ -134,6 +142,9 @@ def tile_metalstmcell_pb_e_kernel(
             tp = psum_m.tile([P, 4, P], F32, tag="a_ps")
             nc.tensor.transpose(tp[:, 0, :], rows_raw[:].bitcast(F32), ident_f32[:])
             nc.scalar.copy(out=rowsT[:], in_=tp[:, 0, :].bitcast(BF16))
+            tb = psum_m.tile([P, P], BF16, tag="a_ps")
+            nc.tensor.transpose(tb[:], beta_raw[:], ident_bf16[:])
+            nc.scalar.copy(out=betaT[:], in_=tb[:])
 
         def spread_row(name, g, bank):
             for q in range(QUARTERS):
@@ -148,17 +159,6 @@ def tile_metalstmcell_pb_e_kernel(
             bank = psum_ln.tile([P, BANK], F32, tag=name)
             spread_row(name, g, bank)
             gate_rows[(name, g)] = bank[:].bitcast(BF16)
-
-        def spread_beta(g):
-            bank = psum_m.tile([P, BANK], F32, tag="a_ps")
-            spread_row("beta", g, bank)
-            beta = gatew.tile([P, H], BF16, tag="beta")
-            nc.scalar.copy(out=beta[:], in_=bank[:].bitcast(BF16))
-            gate_rows[("beta", g)] = beta[:]
-            junk = work.tile([P, H], F32, tag="sq")
-            nbm = stats.tile([P, 1], F32, tag="nbm")
-            nc.scalar.activation(out=junk[:], in_=beta[:], func=ACT.Copy, scale=-0.5 / H, accum_out=nbm[:])
-            neg_beta_mean[g] = nbm
 
         def prepare_batch_tile(bt):
             h_raw, zh_raw, zb_raw = batch_raw[bt]
@@ -230,12 +230,22 @@ def tile_metalstmcell_pb_e_kernel(
             for half in range(HALVES):
                 cols = slice(half * BANK, (half + 1) * BANK)
                 d_ps = psum_m.tile([P, BANK], F32, tag="d_ps")
+                for j in range(BANK // P):
+                    column = (H // P) * g + (BANK // P) * half + j
+                    nc.tensor.matmul(
+                        d_ps[:, j * P : (j + 1) * P],
+                        lhsT=betaT[:, column : column + 1].to_broadcast([P, P]),
+                        rhs=ident_f32[:],
+                        is_transpose=True,
+                        start=(j == 0),
+                        stop=False,
+                    )
                 for e in range(2):
                     nc.tensor.matmul(
                         d_ps[:],
                         lhsT=zbT[:, bt, g, :, e],
                         rhs=gate_T[("dbT", g)][:, cols, e],
-                        start=(e == 0),
+                        start=False,
                         stop=False,
                     )
                 nc.tensor.matmul(
@@ -268,13 +278,9 @@ def tile_metalstmcell_pb_e_kernel(
             junk2 = stats.tile([P, HALVES], F32, tag="junk2")
             neg_mu = stats.tile([P, 1], F32, tag="neg_mu")
             nc.scalar.activation(
-                out=junk2[:], in_=ysums[k][:], func=ACT.Identity, scale=-1.0 / H,
-                bias=neg_beta_mean[k // NBT][:], accum_out=neg_mu[:],
+                out=junk2[:], in_=ysums[k][:], func=ACT.Copy, scale=-1.0 / H, accum_out=neg_mu[:]
             )
             neg_mus[k] = neg_mu
-
-        def add_bias(k):
-            nc.gpsimd.tensor_tensor(out=ys[k][:], in0=ys[k][:], in1=gate_rows[("beta", k // NBT)], op=ALU.add)
 
         def squares(k):
             sq = work.tile([P, H], F32, tag="sq")
@@ -286,15 +292,13 @@ def tile_metalstmcell_pb_e_kernel(
 
         def inverse_std(k):
             var_eps = stats.tile([P, 1], F32, tag="var_eps")
-            nc.gpsimd.tensor_scalar(
-                out=var_eps[:], in0=ssqs[k][:], scalar1=1.0 / H, scalar2=EPS, op0=ALU.mult, op1=ALU.add
-            )
+            nc.scalar.activation(out=var_eps[:], in_=ssqs[k][:], func=ACT.Identity, scale=1.0 / H, bias=eps_col[:])
             rstd = stats.tile([P, 1], F32, tag="rstd")
             nc.gpsimd.tensor_tensor(out=rstd[:], in0=var_eps[:], in1=neg_half[:], op=ALU.pow)
             rstds[k] = rstd
 
         def centre_and_gain(k):
-            v = work.tile([P, H], F32, tag="v", bufs=3)
+            v = work.tile([P, H], F32, tag="v", bufs=5)
             nc.vector.scalar_tensor_tensor(
                 out=v[:], in0=ys[k][:], scalar=neg_mus[k][:], in1=gate_rows[("lnw", k // NBT)],
                 op0=ALU.add, op1=ALU.mult,
@@ -312,80 +316,78 @@ def tile_metalstmcell_pb_e_kernel(
             dst = keep_a[:, bt, :] if g == 0 else vs[k][:]
             nc.scalar.activation(out=dst, in_=vs[k][:], func=GATE_FUNC[g])
 
-        def cell_on_gpsimd(k):
+        def cell(k):
             g, bt = divmod(k, NBT)
+            rows = slice(bt * P, (bt + 1) * P)
             if g == 1:
                 nc.gpsimd.tensor_tensor(out=keep_b[:, bt, :], in0=vs[k][:], in1=c_sb[:, bt, :], op=ALU.mult)
-            elif g == 3:
-                nc.gpsimd.tensor_tensor(out=vs[k][:], in0=vs[k][:], in1=keep_a[:, bt, :], op=ALU.mult)
+            elif g == 2:
+                nc.gpsimd.tensor_tensor(out=keep_a[:, bt, :], in0=keep_a[:, bt, :], in1=vs[k][:], op=ALU.mult)
+                nc.gpsimd.tensor_tensor(out=keep_b[:, bt, :], in0=keep_b[:, bt, :], in1=keep_a[:, bt, :], op=ALU.add)
+                nc.sync.dma_start(out=c_next[rows, :], in_=keep_b[:, bt, :])
+
+        def hidden(k):
+            g, bt = divmod(k, NBT)
+            if g == 3:
+                nc.vector.tensor_mul(out=vs[k][:], in0=vs[k][:], in1=keep_a[:, bt, :])
                 nc.sync.dma_start(out=h_next[bt * P : (bt + 1) * P, :], in_=vs[k][:])
 
-        def cell_on_vector(k):
+        def cell_tanh(k):
             g, bt = divmod(k, NBT)
             if g == 2:
-                nc.vector.tensor_mul(out=keep_a[:, bt, :], in0=keep_a[:, bt, :], in1=vs[k][:])
-                nc.vector.tensor_add(out=keep_b[:, bt, :], in0=keep_b[:, bt, :], in1=keep_a[:, bt, :])
-                nc.sync.dma_start(out=c_next[bt * P : (bt + 1) * P, :], in_=keep_b[:, bt, :])
                 nc.scalar.activation(out=keep_a[:, bt, :], in_=keep_b[:, bt, :], func=ACT.Tanh)
 
         load_rows()
-        load_scale_planes(0)
-        load_batch_tile(0)
         load_gate_matrices(0)
-        load_px(0, 0)
-        for bt in range(1, NBT):
+        for bt in range(NBT):
             load_batch_tile(bt)
+        load_scale_planes(0)
+        load_gate_words(0)
+        for bt in range(NBT):
             load_px(0, bt)
         nc.sync.dma_start(out=c_sb[:], in_=c.rearrange("(bt p) n -> p bt n", p=P))
         load_scale_planes(1)
         load_gate(1)
 
         prepare_rows()
-        prepare_batch_tile(0)
         prepare_gate_matrix("dhT", 0)
         prepare_gate_matrix("dbT", 0)
+        for bt in range(NBT):
+            prepare_batch_tile(bt)
         scale_matmuls(0)
         other_matmuls(0)
-        spread_beta(0)
         spread_ln_row("lnw", 0)
         spread_ln_row("lnb", 0)
-        prepare_batch_tile(1)
 
         for step in range(UNITS + 3):
             g, bt = divmod(step, NBT)
             if 0 <= step - 1 < UNITS:
-                squares(step - 1)
-            if step + 1 < UNITS:
-                scale_matmuls(step + 1)
+                inverse_std(step - 1)
+            if 0 <= step - 5 < UNITS:
+                cell_tanh(step - 5)
+            if 0 <= step - 3 < UNITS:
+                activate(step - 3)
+                cell(step - 3)
             if step < UNITS:
                 products(step)
             if step + 1 < UNITS:
+                scale_matmuls(step + 1)
                 other_matmuls(step + 1)
             if step < UNITS:
                 mean(step)
-            if 0 <= step - 3 < UNITS:
-                cell_on_gpsimd(step - 3)
-            if 0 <= step - 1 < UNITS:
-                inverse_std(step - 1)
-            if step < UNITS:
-                add_bias(step)
-            if 0 <= step - 2 < UNITS:
-                scale_and_shift(step - 2)
+                squares(step)
             if 0 <= step - 1 < UNITS:
                 centre_and_gain(step - 1)
             if 0 <= step - 2 < UNITS:
-                activate(step - 2)
+                scale_and_shift(step - 2)
             if 0 <= step - 3 < UNITS:
-                cell_on_vector(step - 3)
-            if step + 2 < NBT:
-                prepare_batch_tile(step + 2)
+                hidden(step - 3)
             if 1 <= g and g + 1 < G and bt == 0:
                 load_gate(g + 1)
             if g + 1 < G and bt == 1:
                 prepare_gate_matrix("dhT", g + 1)
             if g + 1 < G and bt == 2:
                 prepare_gate_matrix("dbT", g + 1)
-                spread_beta(g + 1)
             if 1 <= g < G and bt == 0:
                 spread_ln_row("lnw", g)
             if 1 <= g < G and bt == 1:

@@ -77,7 +77,7 @@ def tile_metalstmcell_pb_e_kernel(
         gate_rows = {}
         gate_T = {}
         banks = {}
-        a_sbs, ys, ysums, neg_mus, ssqs, rstds, vs = {}, {}, {}, {}, {}, {}, {}
+        a_sbs, ts, ys, ysums, neg_mus, ssqs, rstds, vs = {}, {}, {}, {}, {}, {}, {}, {}
 
         def load_scale_planes(j):
             for q in range(4):
@@ -125,12 +125,6 @@ def tile_metalstmcell_pb_e_kernel(
                     in_=vector.rearrange("g (q w) -> (g q) w", q=QUARTERS),
                 )
             nc.sync.dma_start(out=beta_raw[0 : G * (H // P), :], in_=db_b.rearrange("g (j w) -> (g j) w", w=P))
-
-        def load_gate(g):
-            load_gate_matrices(g)
-            load_gate_words(g)
-            for bt in range(NBT):
-                load_px(g, bt)
 
         def transpose_pairs(word_blocks, dst):
             tp = psum_m.tile([P, 4, P], F32, tag="a_ps")
@@ -183,14 +177,15 @@ def tile_metalstmcell_pb_e_kernel(
                 in_=grouped[:].rearrange("p s b t -> p (s b t)"),
             )
 
-        def prepare_gate_matrix(name, g):
-            src = gate_raw[g][0 if name == "dhT" else 1]
-            dst = gatew.tile([P, H, 2], BF16, tag=name)
-            src_words = src[:].bitcast(F32)
-            dst_blocks = dst[:].rearrange("p (nt r) e -> p nt (r e)", r=P)
-            for q in range(H // P // 4):
-                transpose_pairs(src_words[:, 4 * q : 4 * q + 4, :], dst_blocks[:, 4 * q : 4 * q + 4, :])
-            gate_T[(name, g)] = dst
+        def prepare_gate_bank(g, i):
+            name = ("dhT", "dbT")[i // 2]
+            q = i % 2
+            if q == 0:
+                fresh = gatew.tile([P, H, 2], BF16, tag=name)
+                gate_T[(name, g)] = fresh
+            src_words = gate_raw[g][i // 2][:].bitcast(F32)
+            dst_blocks = gate_T[(name, g)][:].rearrange("p (nt r) e -> p nt (r e)", r=P)
+            transpose_pairs(src_words[:, 4 * q : 4 * q + 4, :], dst_blocks[:, 4 * q : 4 * q + 4, :])
 
         def scale_matmuls(k):
             g, bt = divmod(k, NBT)
@@ -209,7 +204,7 @@ def tile_metalstmcell_pb_e_kernel(
                 nc.scalar.copy(out=a_sb[:, cols], in_=a_ps[:])
             a_sbs[k] = a_sb
 
-        def other_matmuls(k):
+        def mx_matmuls(k):
             g, bt = divmod(k, NBT)
             for half in range(HALVES):
                 cols = slice(half * BANK, (half + 1) * BANK)
@@ -227,6 +222,9 @@ def tile_metalstmcell_pb_e_kernel(
                         stop=(s == PASSES - 1),
                     )
                 banks[("w", k, half)] = w_ps
+
+        def shift_matmuls(k):
+            g, bt = divmod(k, NBT)
             for half in range(HALVES):
                 cols = slice(half * BANK, (half + 1) * BANK)
                 d_ps = psum_m.tile([P, BANK], F32, tag="d_ps")
@@ -253,18 +251,21 @@ def tile_metalstmcell_pb_e_kernel(
                 )
                 banks[("d", k, half)] = d_ps
 
-        def products(k):
+        def multiply(k):
             t = work.tile([P, H], F32, tag="t")
+            for half in range(HALVES):
+                cols = slice(half * BANK, (half + 1) * BANK)
+                nc.vector.tensor_mul(out=t[:, cols], in0=a_sbs[k][:, cols], in1=banks[("w", k, half)][:])
+            ts[k] = t
+
+        def add_shift(k):
             y = work.tile([P, H], F32, tag="y")
             ysum = stats.tile([P, HALVES], F32, tag="ysum")
             for half in range(HALVES):
                 cols = slice(half * BANK, (half + 1) * BANK)
-                nc.vector.tensor_mul(out=t[:, cols], in0=a_sbs[k][:, cols], in1=banks[("w", k, half)][:])
-            for half in range(HALVES):
-                cols = slice(half * BANK, (half + 1) * BANK)
                 nc.vector.scalar_tensor_tensor(
                     out=y[:, cols],
-                    in0=t[:, cols],
+                    in0=ts[k][:, cols],
                     scalar=1.0,
                     in1=banks[("d", k, half)][:],
                     op0=ALU.mult,
@@ -326,10 +327,10 @@ def tile_metalstmcell_pb_e_kernel(
                 nc.gpsimd.tensor_tensor(out=keep_b[:, bt, :], in0=keep_b[:, bt, :], in1=keep_a[:, bt, :], op=ALU.add)
                 nc.sync.dma_start(out=c_next[rows, :], in_=keep_b[:, bt, :])
 
-        def hidden(k):
+        def hidden(k, engine):
             g, bt = divmod(k, NBT)
             if g == 3:
-                nc.vector.tensor_mul(out=vs[k][:], in0=vs[k][:], in1=keep_a[:, bt, :])
+                engine.tensor_tensor(out=vs[k][:], in0=vs[k][:], in1=keep_a[:, bt, :], op=ALU.mult)
                 nc.sync.dma_start(out=h_next[bt * P : (bt + 1) * P, :], in_=vs[k][:])
 
         def cell_tanh(k):
@@ -343,52 +344,62 @@ def tile_metalstmcell_pb_e_kernel(
             load_batch_tile(bt)
         load_scale_planes(0)
         load_gate_words(0)
-        for bt in range(NBT):
+        load_px(0, 0)
+        load_gate_matrices(1)
+        for bt in range(1, NBT):
             load_px(0, bt)
         nc.sync.dma_start(out=c_sb[:], in_=c.rearrange("(bt p) n -> p bt n", p=P))
         load_scale_planes(1)
-        load_gate(1)
+        load_gate_words(1)
+        for bt in range(NBT):
+            load_px(1, bt)
 
         prepare_rows()
-        prepare_gate_matrix("dhT", 0)
-        prepare_gate_matrix("dbT", 0)
+        for i in range(4):
+            prepare_gate_bank(0, i)
         for bt in range(NBT):
             prepare_batch_tile(bt)
-        scale_matmuls(0)
-        other_matmuls(0)
         spread_ln_row("lnw", 0)
         spread_ln_row("lnb", 0)
+        scale_matmuls(0)
+        mx_matmuls(0)
+        shift_matmuls(0)
 
-        for step in range(UNITS + 3):
+        for step in range(UNITS + 2):
             g, bt = divmod(step, NBT)
             if 0 <= step - 1 < UNITS:
                 inverse_std(step - 1)
-            if 0 <= step - 5 < UNITS:
-                cell_tanh(step - 5)
-            if 0 <= step - 3 < UNITS:
-                activate(step - 3)
-                cell(step - 3)
+            if 0 <= step - 4 < UNITS:
+                cell_tanh(step - 4)
+            if 0 <= step - 2 < UNITS:
+                activate(step - 2)
+                cell(step - 2)
             if step < UNITS:
-                products(step)
+                multiply(step)
+            if 0 <= step - 1 < UNITS:
+                centre_and_gain(step - 1)
+            if step < UNITS:
+                add_shift(step)
+            if 0 <= step - 1 < UNITS:
+                scale_and_shift(step - 1)
             if step + 1 < UNITS:
                 scale_matmuls(step + 1)
-                other_matmuls(step + 1)
+                mx_matmuls(step + 1)
+            if g + 1 < G:
+                prepare_gate_bank(g + 1, bt)
+            if step + 1 < UNITS:
+                shift_matmuls(step + 1)
             if step < UNITS:
                 mean(step)
                 squares(step)
-            if 0 <= step - 1 < UNITS:
-                centre_and_gain(step - 1)
             if 0 <= step - 2 < UNITS:
-                scale_and_shift(step - 2)
-            if 0 <= step - 3 < UNITS:
-                hidden(step - 3)
+                hidden(step - 2, nc.gpsimd if step < UNITS else nc.vector)
+            if g + 2 < G and bt == 0:
+                load_gate_matrices(g + 2)
             if 1 <= g and g + 1 < G and bt == 0:
-                load_gate(g + 1)
-            if g + 1 < G and bt == 1:
-                prepare_gate_matrix("dhT", g + 1)
-            if g + 1 < G and bt == 2:
-                prepare_gate_matrix("dbT", g + 1)
+                load_gate_words(g + 1)
+                for later_bt in range(NBT):
+                    load_px(g + 1, later_bt)
             if 1 <= g < G and bt == 0:
                 spread_ln_row("lnw", g)
-            if 1 <= g < G and bt == 1:
                 spread_ln_row("lnb", g)

@@ -23,6 +23,7 @@ K_PASS = 512
 PASSES = H // K_PASS
 PLANES = 4
 QUARTERS = 4
+MATRICES = ("dh", "zh", "db", "zb")
 ROW_INDEX = {"lnw": 0, "lnb": 1}
 
 FLOPS = 2 * B * G * H * (H + 2 * Z)
@@ -64,13 +65,11 @@ def tile_metalstmcell_pb_e_kernel(
 
         h_codes = const.tile([P, NBT, PASSES * P], U32, align_bytes=64)
         h_scales = const.tile([P, NBT, PASSES * P], U8, align_bytes=64)
-        zhT = const.tile([P, NBT, G, P, 2], BF16)
-        zbT = const.tile([P, NBT, G, P, 2], BF16)
         c_sb = const.tile([P, NBT, H], BF16)
         keep_a = const.tile([P, NBT, H], F32)
         keep_b = const.tile([P, NBT, H], F32)
 
-        batch_raw = {}
+        h_raws = {}
         gate_raw = {}
         gate_mx = {}
         gate_px = {}
@@ -86,22 +85,16 @@ def tile_metalstmcell_pb_e_kernel(
                     in_=w_h_scales[PLANES * j : PLANES * (j + 1), 4 * q : 4 * q + 4, :].bitcast(I32),
                 )
 
-        def load_batch_tile(bt):
-            rows = slice(bt * P, (bt + 1) * P)
+        def load_h(bt):
             h_raw = raw.tile([P, H], BF16, tag="h_raw")
-            nc.sync.dma_start(out=h_raw[:], in_=h[rows, :])
-            zh_raw = raw.tile([P, G, Z], BF16, tag="zh_raw")
-            nc.sync.dma_start(out=zh_raw[:], in_=zh[rows])
-            zb_raw = raw.tile([P, G, Z], BF16, tag="zb_raw")
-            nc.sync.dma_start(out=zb_raw[:], in_=zb[rows])
-            batch_raw[bt] = (h_raw, zh_raw, zb_raw)
+            nc.sync.dma_start(out=h_raw[:], in_=h[bt * P : (bt + 1) * P, :])
+            h_raws[bt] = h_raw
 
         def load_gate_matrices(g):
-            dh_raw = gatew.tile([P, H // P, Z], BF16, tag="dh_raw")
-            nc.sync.dma_start(out=dh_raw[:], in_=dh_w[g].rearrange("(nt p) z -> p nt z", p=P))
-            db_raw = gatew.tile([P, H // P, Z], BF16, tag="db_raw")
-            nc.sync.dma_start(out=db_raw[:], in_=db_w[g].rearrange("(nt p) z -> p nt z", p=P))
-            gate_raw[g] = (dh_raw, db_raw)
+            for name, rows in zip(MATRICES, (dh_w[g], zh[:, g, :], db_w[g], zb[:, g, :])):
+                loaded = gatew.tile([P, rows.shape[0] // P, Z], BF16, tag=name + "_raw")
+                nc.sync.dma_start(out=loaded[:], in_=rows.rearrange("(j p) z -> p j z", p=P))
+                gate_raw[(name, g)] = loaded
 
         def load_gate_words(g):
             words = gatew.tile([P, PASSES, H], U32, tag="words", align_bytes=64)
@@ -154,11 +147,8 @@ def tile_metalstmcell_pb_e_kernel(
             spread_row(name, g, bank)
             gate_rows[(name, g)] = bank[:].bitcast(BF16)
 
-        def prepare_batch_tile(bt):
-            h_raw, zh_raw, zb_raw = batch_raw[bt]
-            transpose_pairs(zh_raw[:].bitcast(F32), zhT[:, bt].rearrange("p g b e -> p g (b e)"))
-            transpose_pairs(zb_raw[:].bitcast(F32), zbT[:, bt].rearrange("p g b e -> p g (b e)"))
-            h_words = h_raw[:].bitcast(F32)
+        def prepare_h(bt):
+            h_words = h_raws[bt][:].bitcast(F32)
             tp = psum_m.tile([P, 4, P], F32, tag="a_ps")
             for s in range(PASSES):
                 for u in range(2):
@@ -177,15 +167,14 @@ def tile_metalstmcell_pb_e_kernel(
                 in_=grouped[:].rearrange("p s b t -> p (s b t)"),
             )
 
-        def prepare_gate_bank(g, i):
-            name = ("dhT", "dbT")[i // 2]
-            q = i % 2
-            if q == 0:
-                fresh = gatew.tile([P, H, 2], BF16, tag=name)
-                gate_T[(name, g)] = fresh
-            src_words = gate_raw[g][i // 2][:].bitcast(F32)
-            dst_blocks = gate_T[(name, g)][:].rearrange("p (nt r) e -> p nt (r e)", r=P)
-            transpose_pairs(src_words[:, 4 * q : 4 * q + 4, :], dst_blocks[:, 4 * q : 4 * q + 4, :])
+        def prepare_gate_matrix(name, g):
+            src_words = gate_raw[(name, g)][:].bitcast(F32)
+            blocks = src_words.shape[1]
+            dst = gatew.tile([P, blocks * P, 2], BF16, tag=name + "T")
+            dst_blocks = dst[:].rearrange("p (j r) e -> p j (r e)", r=P)
+            for q in range(blocks // 4):
+                transpose_pairs(src_words[:, 4 * q : 4 * q + 4, :], dst_blocks[:, 4 * q : 4 * q + 4, :])
+            gate_T[(name, g)] = dst
 
         def scale_matmuls(k):
             g, bt = divmod(k, NBT)
@@ -196,8 +185,8 @@ def tile_metalstmcell_pb_e_kernel(
                 for e in range(2):
                     nc.tensor.matmul(
                         a_ps[:],
-                        lhsT=zhT[:, bt, g, :, e],
-                        rhs=gate_T[("dhT", g)][:, cols, e],
+                        lhsT=gate_T[("zh", g)][:, bt * P : (bt + 1) * P, e],
+                        rhs=gate_T[("dh", g)][:, cols, e],
                         start=(e == 0),
                         stop=(e == 1),
                     )
@@ -241,8 +230,8 @@ def tile_metalstmcell_pb_e_kernel(
                 for e in range(2):
                     nc.tensor.matmul(
                         d_ps[:],
-                        lhsT=zbT[:, bt, g, :, e],
-                        rhs=gate_T[("dbT", g)][:, cols, e],
+                        lhsT=gate_T[("zb", g)][:, bt * P : (bt + 1) * P, e],
+                        rhs=gate_T[("db", g)][:, cols, e],
                         start=False,
                         stop=False,
                     )
@@ -341,12 +330,13 @@ def tile_metalstmcell_pb_e_kernel(
         load_rows()
         load_gate_matrices(0)
         for bt in range(NBT):
-            load_batch_tile(bt)
+            load_h(bt)
         load_scale_planes(0)
         load_gate_words(0)
         load_px(0, 0)
+        load_px(0, 1)
         load_gate_matrices(1)
-        for bt in range(1, NBT):
+        for bt in range(2, NBT):
             load_px(0, bt)
         nc.sync.dma_start(out=c_sb[:], in_=c.rearrange("(bt p) n -> p bt n", p=P))
         load_scale_planes(1)
@@ -355,10 +345,10 @@ def tile_metalstmcell_pb_e_kernel(
             load_px(1, bt)
 
         prepare_rows()
-        for i in range(4):
-            prepare_gate_bank(0, i)
+        for name in MATRICES:
+            prepare_gate_matrix(name, 0)
         for bt in range(NBT):
-            prepare_batch_tile(bt)
+            prepare_h(bt)
         spread_ln_row("lnw", 0)
         spread_ln_row("lnb", 0)
         scale_matmuls(0)
@@ -386,7 +376,7 @@ def tile_metalstmcell_pb_e_kernel(
                 scale_matmuls(step + 1)
                 mx_matmuls(step + 1)
             if g + 1 < G:
-                prepare_gate_bank(g + 1, bt)
+                prepare_gate_matrix(MATRICES[bt], g + 1)
             if step + 1 < UNITS:
                 shift_matmuls(step + 1)
             if step < UNITS:

@@ -28,6 +28,7 @@ ROW_INDEX = {"lnw": 0, "lnb": 1}
 
 FLOPS = 2 * B * G * H * (H + 2 * Z)
 
+PX_ON_TENSOR = G - 1
 GATE_FUNC = (ACT.Sigmoid, ACT.Sigmoid, ACT.Tanh, ACT.Sigmoid)
 
 
@@ -59,9 +60,10 @@ def tile_metalstmcell_pb_e_kernel(
         rows_raw = const.tile([P, 2 * P], BF16)
         nc.vector.memset(rows_raw[:], 0.0)
         rowsT = const.tile([P, 2 * P], BF16)
-        beta_raw = const.tile([P, P], BF16)
-        nc.vector.memset(beta_raw[:], 0.0)
-        betaT = const.tile([P, P], F32)
+        ones = const.tile([P, P], BF16)
+        nc.vector.memset(ones[:], 1.0)
+        beta_rows = const.tile([P, G, H], BF16)
+        nc.vector.memset(beta_rows[:], 0.0)
 
         h_codes = const.tile([P, NBT, PASSES * P], U32, align_bytes=64)
         h_scales = const.tile([P, NBT, PASSES * P], U8, align_bytes=64)
@@ -117,7 +119,7 @@ def tile_metalstmcell_pb_e_kernel(
                     out=rows_raw[G * QUARTERS * i : G * QUARTERS * (i + 1), :],
                     in_=vector.rearrange("g (q w) -> (g q) w", q=QUARTERS),
                 )
-            nc.sync.dma_start(out=beta_raw[0 : G * (H // P), :], in_=db_b.rearrange("g (j w) -> (g j) w", w=P))
+            nc.sync.dma_start(out=beta_rows[0:1, :, :], in_=db_b.rearrange("(o g) n -> o g n", o=1))
 
         def transpose_pairs(word_blocks, dst):
             tp = psum_m.tile([P, 4, P], F32, tag="a_ps")
@@ -129,9 +131,6 @@ def tile_metalstmcell_pb_e_kernel(
             tp = psum_m.tile([P, 4, P], F32, tag="a_ps")
             nc.tensor.transpose(tp[:, 0, :], rows_raw[:].bitcast(F32), ident_f32[:])
             nc.scalar.copy(out=rowsT[:], in_=tp[:, 0, :].bitcast(BF16))
-            tb = psum_m.tile([P, P], BF16, tag="a_ps")
-            nc.tensor.transpose(tb[:], beta_raw[:], ident_bf16[:])
-            nc.scalar.copy(out=betaT[:], in_=tb[:])
 
         def spread_row(name, g, bank):
             for q in range(QUARTERS):
@@ -217,27 +216,19 @@ def tile_metalstmcell_pb_e_kernel(
             for half in range(HALVES):
                 cols = slice(half * BANK, (half + 1) * BANK)
                 d_ps = psum_m.tile([P, BANK], F32, tag="d_ps")
-                for j in range(BANK // P):
-                    column = (H // P) * g + (BANK // P) * half + j
-                    nc.tensor.matmul(
-                        d_ps[:, j * P : (j + 1) * P],
-                        lhsT=betaT[:, column : column + 1].to_broadcast([P, P]),
-                        rhs=ident_f32[:],
-                        is_transpose=True,
-                        start=(j == 0),
-                        stop=False,
-                    )
+                nc.tensor.matmul(d_ps[:], lhsT=ones[:], rhs=beta_rows[:, g, cols], start=True, stop=False)
                 for e in range(2):
                     nc.tensor.matmul(
                         d_ps[:],
                         lhsT=gate_T[("zb", g)][:, bt * P : (bt + 1) * P, e],
                         rhs=gate_T[("db", g)][:, cols, e],
                         start=False,
-                        stop=False,
+                        stop=(e == 1 and g != PX_ON_TENSOR),
                     )
-                nc.tensor.matmul(
-                    d_ps[:], lhsT=ident_bf16[:], rhs=gate_px[g][:, bt, cols], start=False, stop=True
-                )
+                if g == PX_ON_TENSOR:
+                    nc.tensor.matmul(
+                        d_ps[:], lhsT=ident_bf16[:], rhs=gate_px[g][:, bt, cols], start=False, stop=True
+                    )
                 banks[("d", k, half)] = d_ps
 
         def multiply(k):
@@ -246,6 +237,11 @@ def tile_metalstmcell_pb_e_kernel(
                 cols = slice(half * BANK, (half + 1) * BANK)
                 nc.vector.tensor_mul(out=t[:, cols], in0=a_sbs[k][:, cols], in1=banks[("w", k, half)][:])
             ts[k] = t
+
+        def add_px(k):
+            g, bt = divmod(k, NBT)
+            if g != PX_ON_TENSOR:
+                nc.gpsimd.tensor_tensor(out=ts[k][:], in0=ts[k][:], in1=gate_px[g][:, bt, :], op=ALU.add)
 
         def add_shift(k):
             y = work.tile([P, H], F32, tag="y")
@@ -351,45 +347,48 @@ def tile_metalstmcell_pb_e_kernel(
             prepare_h(bt)
         spread_ln_row("lnw", 0)
         spread_ln_row("lnb", 0)
-        scale_matmuls(0)
-        mx_matmuls(0)
-        shift_matmuls(0)
 
-        for step in range(UNITS + 2):
+        def on(k):
+            return 0 <= k < UNITS
+
+        for step in range(-2, UNITS + 4):
             g, bt = divmod(step, NBT)
-            if 0 <= step - 1 < UNITS:
+            if on(step - 1):
+                mean(step - 1)
+                squares(step - 1)
                 inverse_std(step - 1)
-            if 0 <= step - 4 < UNITS:
-                cell_tanh(step - 4)
-            if 0 <= step - 2 < UNITS:
-                activate(step - 2)
-                cell(step - 2)
-            if step < UNITS:
-                multiply(step)
-            if 0 <= step - 1 < UNITS:
+            if on(step + 1):
+                multiply(step + 1)
+                add_px(step + 1)
+            if on(step - 1):
                 centre_and_gain(step - 1)
-            if step < UNITS:
+            if on(step):
                 add_shift(step)
-            if 0 <= step - 1 < UNITS:
+            if on(step - 1):
                 scale_and_shift(step - 1)
-            if step + 1 < UNITS:
-                scale_matmuls(step + 1)
-                mx_matmuls(step + 1)
-            if g + 1 < G:
-                prepare_gate_matrix(MATRICES[bt], g + 1)
-            if step + 1 < UNITS:
+            if on(step + 2):
+                scale_matmuls(step + 2)
+            if on(step - 2):
+                activate(step - 2)
+            if on(step - 4):
+                cell_tanh(step - 4)
+            if on(step + 2):
+                mx_matmuls(step + 2)
+            if 0 <= g and g + 1 < G:
+                for name in (("dh",), ("zh", "zb"), ("db",), ())[bt]:
+                    prepare_gate_matrix(name, g + 1)
+            if 1 <= g < G and bt == 0:
+                spread_ln_row("lnw", g)
+            if on(step + 1):
                 shift_matmuls(step + 1)
-            if step < UNITS:
-                mean(step)
-                squares(step)
-            if 0 <= step - 2 < UNITS:
-                hidden(step - 2, nc.gpsimd if step < UNITS else nc.vector)
-            if g + 2 < G and bt == 0:
+            if 1 <= g < G and bt == 0:
+                spread_ln_row("lnb", g)
+            if on(step - 3):
+                cell(step - 3)
+                hidden(step - 3, nc.gpsimd if step < UNITS else nc.vector)
+            if 0 <= g and g + 2 < G and bt == 0:
                 load_gate_matrices(g + 2)
             if 1 <= g and g + 1 < G and bt == 0:
                 load_gate_words(g + 1)
                 for later_bt in range(NBT):
                     load_px(g + 1, later_bt)
-            if 1 <= g < G and bt == 0:
-                spread_ln_row("lnw", g)
-                spread_ln_row("lnb", g)

@@ -92,20 +92,24 @@ def tile_metalstmcell_pb_e_kernel(
             nc.sync.dma_start(out=h_raw[:], in_=h[bt * P : (bt + 1) * P, :])
             h_raws[bt] = h_raw
 
-        def load_gate_matrices(g):
-            for name, rows in zip(MATRICES, (dh_w[g], zh[:, g, :], db_w[g], zb[:, g, :])):
+        def load_gate_matrices(g, names):
+            sources = {"dh": dh_w[g], "zh": zh[:, g, :], "db": db_w[g], "zb": zb[:, g, :]}
+            for name in names:
+                rows = sources[name]
                 loaded = gatew.tile([P, rows.shape[0] // P, Z], BF16, tag=name + "_raw")
                 nc.sync.dma_start(out=loaded[:], in_=rows.rearrange("(j p) z -> p j z", p=P))
                 gate_raw[(name, g)] = loaded
 
         def load_gate_words(g):
             words = gatew.tile([P, PASSES, H], U32, tag="words", align_bytes=64)
-            nc.sync.dma_start(
-                out=words[:].bitcast(I32),
-                in_=w_h_words[PASSES * g : PASSES * (g + 1)]
-                .rearrange("s p n t -> p s (n t)")
-                .bitcast(I32),
-            )
+            for half in range(HALVES):
+                cols = slice(half * BANK, (half + 1) * BANK)
+                nc.sync.dma_start(
+                    out=words[:, :, cols].bitcast(I32),
+                    in_=w_h_words[PASSES * g : PASSES * (g + 1), :, cols, :]
+                    .rearrange("s p n t -> p s (n t)")
+                    .bitcast(I32),
+                )
             gate_mx[g] = words
             px_sb = gatew.tile([P, NBT, H], BF16, tag="px_sb")
             gate_px[g] = px_sb
@@ -119,13 +123,15 @@ def tile_metalstmcell_pb_e_kernel(
                     out=rows_raw[G * QUARTERS * i : G * QUARTERS * (i + 1), :],
                     in_=vector.rearrange("g (q w) -> (g q) w", q=QUARTERS),
                 )
-            nc.sync.dma_start(out=beta_rows[0:1, :, :], in_=db_b.rearrange("(o g) n -> o g n", o=1))
 
-        def transpose_pairs(word_blocks, dst):
-            tp = psum_m.tile([P, 4, P], F32, tag="a_ps")
+        def transpose_pairs(word_blocks, dst, tag, on_vector):
+            tp = psum_m.tile([P, 4, P], F32, tag=tag)
             for j in range(4):
                 nc.tensor.transpose(tp[:, j, :], word_blocks[:, j, :], ident_f32[:])
-            nc.scalar.copy(out=dst, in_=tp[:].bitcast(BF16))
+            if on_vector:
+                nc.vector.tensor_copy(out=dst, in_=tp[:].bitcast(BF16))
+            else:
+                nc.scalar.copy(out=dst, in_=tp[:].bitcast(BF16))
 
         def prepare_rows():
             tp = psum_m.tile([P, 4, P], F32, tag="a_ps")
@@ -146,9 +152,9 @@ def tile_metalstmcell_pb_e_kernel(
             spread_row(name, g, bank)
             gate_rows[(name, g)] = bank[:].bitcast(BF16)
 
-        def prepare_h(bt):
+        def prepare_h(bt, tag="a_ps"):
             h_words = h_raws[bt][:].bitcast(F32)
-            tp = psum_m.tile([P, 4, P], F32, tag="a_ps")
+            tp = psum_m.tile([P, 4, P], F32, tag=tag)
             for s in range(PASSES):
                 for u in range(2):
                     nc.tensor.transpose(
@@ -166,13 +172,13 @@ def tile_metalstmcell_pb_e_kernel(
                 in_=grouped[:].rearrange("p s b t -> p (s b t)"),
             )
 
-        def prepare_gate_matrix(name, g):
+        def prepare_gate_matrix(name, g, tags=("a_ps", "a_ps"), on_vector=False):
             src_words = gate_raw[(name, g)][:].bitcast(F32)
             blocks = src_words.shape[1]
             dst = gatew.tile([P, blocks * P, 2], BF16, tag=name + "T")
             dst_blocks = dst[:].rearrange("p (j r) e -> p j (r e)", r=P)
             for q in range(blocks // 4):
-                transpose_pairs(src_words[:, 4 * q : 4 * q + 4, :], dst_blocks[:, 4 * q : 4 * q + 4, :])
+                transpose_pairs(src_words[:, 4 * q : 4 * q + 4, :], dst_blocks[:, 4 * q : 4 * q + 4, :], tags[q], on_vector)
             gate_T[(name, g)] = dst
 
         def scale_matmuls(k):
@@ -323,30 +329,30 @@ def tile_metalstmcell_pb_e_kernel(
             if g == 2:
                 nc.scalar.activation(out=keep_a[:, bt, :], in_=keep_b[:, bt, :], func=ACT.Tanh)
 
-        load_rows()
-        load_gate_matrices(0)
-        for bt in range(NBT):
-            load_h(bt)
+        load_gate_matrices(0, ("zh", "dh"))
+        load_h(0)
         load_scale_planes(0)
         load_gate_words(0)
+        load_h(1)
+        load_gate_matrices(0, ("zb", "db"))
+        load_rows()
+        nc.sync.dma_start(out=beta_rows[0:1, :, :], in_=db_b.rearrange("(o g) n -> o g n", o=1))
         load_px(0, 0)
+        load_h(2)
         load_px(0, 1)
-        load_gate_matrices(1)
-        for bt in range(2, NBT):
-            load_px(0, bt)
+        load_h(3)
+        load_px(0, 2)
+        load_px(0, 3)
+        load_gate_matrices(1, ("dh", "zh", "zb", "db"))
         nc.sync.dma_start(out=c_sb[:], in_=c.rearrange("(bt p) n -> p bt n", p=P))
         load_scale_planes(1)
         load_gate_words(1)
         for bt in range(NBT):
             load_px(1, bt)
 
-        prepare_rows()
-        for name in MATRICES:
-            prepare_gate_matrix(name, 0)
-        for bt in range(NBT):
-            prepare_h(bt)
-        spread_ln_row("lnw", 0)
-        spread_ln_row("lnb", 0)
+        prepare_gate_matrix("zh", 0, ("a_ps",), True)
+        prepare_gate_matrix("dh", 0, ("w_ps", "d_ps"))
+        prepare_h(0, "a_ps")
 
         def on(k):
             return 0 <= k < UNITS
@@ -374,20 +380,26 @@ def tile_metalstmcell_pb_e_kernel(
                 cell_tanh(step - 4)
             if on(step + 2):
                 mx_matmuls(step + 2)
+            if step == -1:
+                prepare_gate_matrix("zb", 0, ("a_ps",), True)
+                prepare_gate_matrix("db", 0, ("d_ps", "d_ps"))
+                prepare_rows()
+            if 1 <= step + 3 < NBT:
+                prepare_h(step + 3)
             if 0 <= g and g + 1 < G:
                 for name in (("dh",), ("zh", "zb"), ("db",), ())[bt]:
                     prepare_gate_matrix(name, g + 1)
-            if 1 <= g < G and bt == 0:
+            if 0 <= g < G and bt == 0:
                 spread_ln_row("lnw", g)
             if on(step + 1):
                 shift_matmuls(step + 1)
-            if 1 <= g < G and bt == 0:
+            if 0 <= g < G and bt == 0:
                 spread_ln_row("lnb", g)
             if on(step - 3):
                 cell(step - 3)
-                hidden(step - 3, nc.gpsimd if step < UNITS else nc.vector)
+                hidden(step - 3, nc.gpsimd if step < UNITS + 1 else nc.vector)
             if 0 <= g and g + 2 < G and bt == 0:
-                load_gate_matrices(g + 2)
+                load_gate_matrices(g + 2, ("dh", "zh", "zb", "db"))
             if 1 <= g and g + 1 < G and bt == 0:
                 load_gate_words(g + 1)
                 for later_bt in range(NBT):

@@ -129,14 +129,14 @@ def tile_metalstmcell_pb_e_kernel(
             for j in range(4):
                 nc.tensor.transpose(tp[:, j, :], word_blocks[:, j, :], ident_f32[:])
             if on_vector:
-                nc.vector.tensor_copy(out=dst, in_=tp[:].bitcast(BF16))
+                nc.vector.tensor_copy(out=dst.bitcast(F32), in_=tp[:])
             else:
-                nc.scalar.copy(out=dst, in_=tp[:].bitcast(BF16))
+                nc.scalar.copy(out=dst.bitcast(F32), in_=tp[:])
 
         def prepare_rows():
             tp = psum_m.tile([P, 4, P], F32, tag="a_ps")
             nc.tensor.transpose(tp[:, 0, :], rows_raw[:].bitcast(F32), ident_f32[:])
-            nc.scalar.copy(out=rowsT[:], in_=tp[:, 0, :].bitcast(BF16))
+            nc.scalar.copy(out=rowsT[:].bitcast(F32), in_=tp[:, 0, :])
 
         def spread_row(name, g, bank):
             for q in range(QUARTERS):

@@ -30,6 +30,7 @@ FLOPS = 2 * B * G * H * (H + 2 * Z)
 
 PX_ON_TENSOR = G - 1
 GATE_FUNC = (ACT.Sigmoid, ACT.Sigmoid, ACT.Tanh, ACT.Sigmoid)
+ORDER = (1, 0, 2, 3)
 
 
 def tile_metalstmcell_pb_e_kernel(
@@ -93,7 +94,8 @@ def tile_metalstmcell_pb_e_kernel(
             h_raws[bt] = h_raw
 
         def load_gate_matrices(g, names):
-            sources = {"dh": dh_w[g], "zh": zh[:, g, :], "db": db_w[g], "zb": zb[:, g, :]}
+            real = ORDER[g]
+            sources = {"dh": dh_w[real], "zh": zh[:, real, :], "db": db_w[real], "zb": zb[:, real, :]}
             for name in names:
                 rows = sources[name]
                 loaded = gatew.tile([P, rows.shape[0] // P, Z], BF16, tag=name + "_raw")
@@ -106,7 +108,7 @@ def tile_metalstmcell_pb_e_kernel(
                 cols = slice(half * BANK, (half + 1) * BANK)
                 nc.sync.dma_start(
                     out=words[:, :, cols].bitcast(I32),
-                    in_=w_h_words[PASSES * g : PASSES * (g + 1), :, cols, :]
+                    in_=w_h_words[PASSES * ORDER[g] : PASSES * (ORDER[g] + 1), :, cols, :]
                     .rearrange("s p n t -> p s (n t)")
                     .bitcast(I32),
                 )
@@ -115,7 +117,7 @@ def tile_metalstmcell_pb_e_kernel(
             gate_px[g] = px_sb
 
         def load_px(g, bt):
-            nc.sync.dma_start(out=gate_px[g][:, bt, :], in_=px[bt * P : (bt + 1) * P, g, :])
+            nc.sync.dma_start(out=gate_px[g][:, bt, :], in_=px[bt * P : (bt + 1) * P, ORDER[g], :])
 
         def load_rows():
             for i, vector in enumerate((ln_w, ln_b)):
@@ -140,7 +142,7 @@ def tile_metalstmcell_pb_e_kernel(
 
         def spread_row(name, g, bank):
             for q in range(QUARTERS):
-                r = G * QUARTERS * ROW_INDEX[name] + QUARTERS * g + q
+                r = G * QUARTERS * ROW_INDEX[name] + QUARTERS * ORDER[g] + q
                 nc.tensor.transpose(
                     bank[:, q * P : (q + 1) * P],
                     rowsT[:].bitcast(F32)[:, r : r + 1].to_broadcast([P, P]),
@@ -204,7 +206,7 @@ def tile_metalstmcell_pb_e_kernel(
                 cols = slice(half * BANK, (half + 1) * BANK)
                 w_ps = psum_m.tile([P, BANK], F32, tag="w_ps")
                 for s in range(PASSES):
-                    group = PASSES * g + s
+                    group = PASSES * ORDER[g] + s
                     row0 = 4 * (group % PLANES)
                     nc.tensor.matmul_mx(
                         out=w_ps[:],
@@ -222,7 +224,7 @@ def tile_metalstmcell_pb_e_kernel(
             for half in range(HALVES):
                 cols = slice(half * BANK, (half + 1) * BANK)
                 d_ps = psum_m.tile([P, BANK], F32, tag="d_ps")
-                nc.tensor.matmul(d_ps[:], lhsT=ones[:], rhs=beta_rows[:, g, cols], start=True, stop=False)
+                nc.tensor.matmul(d_ps[:], lhsT=ones[:], rhs=beta_rows[:, ORDER[g], cols], start=True, stop=False)
                 for e in range(2):
                     nc.tensor.matmul(
                         d_ps[:],
@@ -305,16 +307,24 @@ def tile_metalstmcell_pb_e_kernel(
 
         def activate(k):
             g, bt = divmod(k, NBT)
+            g = ORDER[g]
             dst = keep_a[:, bt, :] if g == 0 else vs[k][:]
             nc.scalar.activation(out=dst, in_=vs[k][:], func=GATE_FUNC[g])
 
         def cell(k):
             g, bt = divmod(k, NBT)
+            g = ORDER[g]
             rows = slice(bt * P, (bt + 1) * P)
             if g == 1:
                 nc.gpsimd.tensor_tensor(out=keep_b[:, bt, :], in0=vs[k][:], in1=c_sb[:, bt, :], op=ALU.mult)
             elif g == 2:
                 nc.gpsimd.tensor_tensor(out=keep_a[:, bt, :], in0=keep_a[:, bt, :], in1=vs[k][:], op=ALU.mult)
+
+        def cell_sum(k):
+            g, bt = divmod(k, NBT)
+            g = ORDER[g]
+            rows = slice(bt * P, (bt + 1) * P)
+            if g == 2:
                 nc.gpsimd.tensor_tensor(out=keep_b[:, bt, :], in0=keep_b[:, bt, :], in1=keep_a[:, bt, :], op=ALU.add)
                 nc.sync.dma_start(out=c_next[rows, :], in_=keep_b[:, bt, :])
 
@@ -362,6 +372,9 @@ def tile_metalstmcell_pb_e_kernel(
             if on(step - 1):
                 mean(step - 1)
                 squares(step - 1)
+            if on(step - 3):
+                cell(step - 3)
+            if on(step - 1):
                 inverse_std(step - 1)
             if on(step + 1):
                 multiply(step + 1)
@@ -376,8 +389,8 @@ def tile_metalstmcell_pb_e_kernel(
                 scale_matmuls(step + 2)
             if on(step - 2):
                 activate(step - 2)
-            if on(step - 4):
-                cell_tanh(step - 4)
+            if on(step - 5):
+                cell_tanh(step - 5)
             if on(step + 2):
                 mx_matmuls(step + 2)
             if step == -1:
@@ -396,7 +409,7 @@ def tile_metalstmcell_pb_e_kernel(
             if 0 <= g < G and bt == 0:
                 spread_ln_row("lnb", g)
             if on(step - 3):
-                cell(step - 3)
+                cell_sum(step - 3)
                 hidden(step - 3, nc.gpsimd if step < UNITS + 1 else nc.vector)
             if 0 <= g and g + 2 < G and bt == 0:
                 load_gate_matrices(g + 2, ("dh", "zh", "zb", "db"))

@@ -30,6 +30,7 @@ FLOPS = 2 * B * G * H * (H + 2 * Z)
 
 PX_ON_TENSOR = G - 1
 GATE_FUNC = (ACT.Sigmoid, ACT.Sigmoid, ACT.Tanh, ACT.Sigmoid)
+WEIGHTS = ("dh", "db")
 ORDER = (1, 0, 2, 3)
 
 
@@ -59,12 +60,12 @@ def tile_metalstmcell_pb_e_kernel(
         nc.gpsimd.memset(eps_col[:], EPS)
 
         rows_raw = const.tile([P, 2 * P], BF16)
-        nc.vector.memset(rows_raw[:], 0.0)
+        nc.vector.memset(rows_raw[:].bitcast(F32), 0.0)
         rowsT = const.tile([P, 2 * P], BF16)
         ones = const.tile([P, P], BF16)
         nc.vector.memset(ones[:], 1.0)
         beta_rows = const.tile([P, G, H], BF16)
-        nc.vector.memset(beta_rows[:], 0.0)
+        nc.vector.memset(beta_rows[:].bitcast(F32), 0.0)
 
         h_codes = const.tile([P, NBT, PASSES * P], U32, align_bytes=64)
         h_scales = const.tile([P, NBT, PASSES * P], U8, align_bytes=64)
@@ -99,7 +100,13 @@ def tile_metalstmcell_pb_e_kernel(
             for name in names:
                 rows = sources[name]
                 loaded = gatew.tile([P, rows.shape[0] // P, Z], BF16, tag=name + "_raw")
-                nc.sync.dma_start(out=loaded[:], in_=rows.rearrange("(j p) z -> p j z", p=P))
+                if name in WEIGHTS:
+                    nc.sync.dma_start(
+                        out=loaded[:].rearrange("p (q t) z -> p q (t z)", t=4),
+                        in_=rows.rearrange("(q p t) z -> p q (t z)", p=P, t=4),
+                    )
+                else:
+                    nc.sync.dma_start(out=loaded[:], in_=rows.rearrange("(j p) z -> p j z", p=P))
                 gate_raw[(name, g)] = loaded
 
         def load_gate_words(g):
@@ -126,14 +133,18 @@ def tile_metalstmcell_pb_e_kernel(
                     in_=vector.rearrange("g (q w) -> (g q) w", q=QUARTERS),
                 )
 
-        def transpose_pairs(word_blocks, dst, tag, on_vector):
+        def transpose_pairs(word_blocks, dst, tag, on_vector, interleaved):
             tp = psum_m.tile([P, 4, P], F32, tag=tag)
             for j in range(4):
                 nc.tensor.transpose(tp[:, j, :], word_blocks[:, j, :], ident_f32[:])
+            source = tp[:].rearrange("p t r -> p r t") if interleaved else tp[:]
+            target = dst.bitcast(F32)
+            if interleaved:
+                target = target.rearrange("p t r -> p (t r)").rearrange("p (r t) -> p r t", t=4)
             if on_vector:
-                nc.vector.tensor_copy(out=dst.bitcast(F32), in_=tp[:])
+                nc.vector.tensor_copy(out=target, in_=source)
             else:
-                nc.scalar.copy(out=dst.bitcast(F32), in_=tp[:])
+                nc.scalar.copy(out=target, in_=source)
 
         def prepare_rows():
             tp = psum_m.tile([P, 4, P], F32, tag="a_ps")
@@ -180,7 +191,7 @@ def tile_metalstmcell_pb_e_kernel(
             dst = gatew.tile([P, blocks * P, 2], BF16, tag=name + "T")
             dst_blocks = dst[:].rearrange("p (j r) e -> p j (r e)", r=P)
             for q in range(blocks // 4):
-                transpose_pairs(src_words[:, 4 * q : 4 * q + 4, :], dst_blocks[:, 4 * q : 4 * q + 4, :], tags[q], on_vector)
+                transpose_pairs(src_words[:, 4 * q : 4 * q + 4, :], dst_blocks[:, 4 * q : 4 * q + 4, :], tags[q], on_vector, name in WEIGHTS)
             gate_T[(name, g)] = dst
 
         def scale_matmuls(k):
@@ -339,18 +350,17 @@ def tile_metalstmcell_pb_e_kernel(
             if g == 2:
                 nc.scalar.activation(out=keep_a[:, bt, :], in_=keep_b[:, bt, :], func=ACT.Tanh)
 
+        for bt in range(NBT):
+            load_h(bt)
         load_gate_matrices(0, ("zh", "dh"))
-        load_h(0)
         load_scale_planes(0)
         load_gate_words(0)
-        load_h(1)
-        load_gate_matrices(0, ("zb", "db"))
-        load_rows()
-        nc.sync.dma_start(out=beta_rows[0:1, :, :], in_=db_b.rearrange("(o g) n -> o g n", o=1))
+        load_gate_matrices(0, ("zb",))
         load_px(0, 0)
-        load_h(2)
+        load_gate_matrices(0, ("db",))
+        nc.sync.dma_start(out=beta_rows[0:1, :, :], in_=db_b.rearrange("(o g) n -> o g n", o=1))
+        load_rows()
         load_px(0, 1)
-        load_h(3)
         load_px(0, 2)
         load_px(0, 3)
         load_gate_matrices(1, ("dh", "zh", "zb", "db"))
@@ -360,9 +370,12 @@ def tile_metalstmcell_pb_e_kernel(
         for bt in range(NBT):
             load_px(1, bt)
 
-        prepare_gate_matrix("zh", 0, ("a_ps",), True)
-        prepare_gate_matrix("dh", 0, ("w_ps", "d_ps"))
         prepare_h(0, "a_ps")
+        prepare_h(1, "a_ps")
+        prepare_h(2, "w_ps")
+        prepare_h(3, "w_ps")
+        prepare_gate_matrix("zh", 0, ("d_ps",))
+        prepare_gate_matrix("dh", 0, ("d_ps", "a_ps"))
 
         def on(k):
             return 0 <= k < UNITS
@@ -397,8 +410,6 @@ def tile_metalstmcell_pb_e_kernel(
                 prepare_gate_matrix("zb", 0, ("a_ps",), True)
                 prepare_gate_matrix("db", 0, ("d_ps", "d_ps"))
                 prepare_rows()
-            if 1 <= step + 3 < NBT:
-                prepare_h(step + 3)
             if 0 <= g and g + 1 < G:
                 for name in (("dh",), ("zh", "zb"), ("db",), ())[bt]:
                     prepare_gate_matrix(name, g + 1)

@@ -59,6 +59,9 @@ def tile_metalstmcell_pb_e_kernel(
         eps_col = const.tile([P, 1], F32)
         nc.gpsimd.memset(eps_col[:], EPS)
 
+        warm = const.tile([P, 1], F32)
+        nc.scalar.activation(out=warm[:], in_=eps_col[:], func=ACT.Sigmoid)
+
         rows_raw = const.tile([P, 2 * P], BF16)
         nc.vector.memset(rows_raw[:].bitcast(F32), 0.0)
         rowsT = const.tile([P, 2 * P], BF16)

@@ -322,17 +322,18 @@ def tile_metalstmcell_pb_e_kernel(
         def activate(k):
             g, bt = divmod(k, NBT)
             g = ORDER[g]
-            dst = keep_a[:, bt, :] if g == 0 else vs[k][:]
+            dst = {0: keep_a[:, bt, :], 1: keep_b[:, bt, :]}.get(g, vs[k][:])
             nc.scalar.activation(out=dst, in_=vs[k][:], func=GATE_FUNC[g])
 
         def cell(k):
             g, bt = divmod(k, NBT)
             g = ORDER[g]
             rows = slice(bt * P, (bt + 1) * P)
-            if g == 1:
-                nc.gpsimd.tensor_tensor(out=keep_b[:, bt, :], in0=vs[k][:], in1=c_sb[:, bt, :], op=ALU.mult)
-            elif g == 2:
+            if g == 2:
                 nc.gpsimd.tensor_tensor(out=keep_a[:, bt, :], in0=keep_a[:, bt, :], in1=vs[k][:], op=ALU.mult)
+
+        def forget(bt):
+            nc.gpsimd.tensor_tensor(out=keep_b[:, bt, :], in0=keep_b[:, bt, :], in1=c_sb[:, bt, :], op=ALU.mult)
 
         def cell_sum(k):
             g, bt = divmod(k, NBT)
@@ -390,6 +391,8 @@ def tile_metalstmcell_pb_e_kernel(
                 squares(step - 1)
             if on(step - 3):
                 cell(step - 3)
+            if 3 <= step < 3 + 2 * NBT and (step - 3) % 2 == 0:
+                forget((step - 3) // 2)
             if on(step - 1):
                 inverse_std(step - 1)
             if on(step + 1):
@@ -413,9 +416,13 @@ def tile_metalstmcell_pb_e_kernel(
                 prepare_gate_matrix("zb", 0, ("a_ps",), True)
                 prepare_gate_matrix("db", 0, ("d_ps", "d_ps"))
                 prepare_rows()
+            if step == 0:
+                prepare_gate_matrix("dh", 1)
             if 0 <= g and g + 1 < G:
-                for name in (("dh",), ("zh", "zb"), ("db",), ())[bt]:
+                for name in ((), ("zh", "zb"), ("db",), ())[bt]:
                     prepare_gate_matrix(name, g + 1)
+            if 0 <= g and g + 2 < G and bt == NBT - 1:
+                prepare_gate_matrix("dh", g + 2)
             if 0 <= g < G and bt == 0:
                 spread_ln_row("lnw", g)
             if on(step + 1):

@@ -255,7 +255,7 @@ def tile_metalstmcell_pb_e_kernel(
 
         def multiply(k):
             t = work.tile([P, H], F32, tag="t")
-            for half in range(HALVES):
+            for half in reversed(range(HALVES)):
                 cols = slice(half * BANK, (half + 1) * BANK)
                 nc.vector.tensor_mul(out=t[:, cols], in0=a_sbs[k][:, cols], in1=banks[("w", k, half)][:])
             ts[k] = t
@@ -268,7 +268,7 @@ def tile_metalstmcell_pb_e_kernel(
         def add_shift(k):
             y = work.tile([P, H], F32, tag="y")
             ysum = stats.tile([P, HALVES], F32, tag="ysum")
-            for half in range(HALVES):
+            for half in reversed(range(HALVES)):
                 cols = slice(half * BANK, (half + 1) * BANK)
                 nc.vector.scalar_tensor_tensor(
                     out=y[:, cols],

@@ -237,7 +237,7 @@ def tile_metalstmcell_pb_e_kernel(
             g, bt = divmod(k, NBT)
             for half in range(HALVES):
                 cols = slice(half * BANK, (half + 1) * BANK)
-                d_ps = psum_m.tile([P, BANK], F32, tag="d_ps")
+                d_ps = psum_m.tile([P, BANK], F32, tag="a_ps" if k == UNITS - 1 else "d_ps")
                 nc.tensor.matmul(d_ps[:], lhsT=ones[:], rhs=beta_rows[:, ORDER[g], cols], start=True, stop=False)
                 for e in range(2):
                     nc.tensor.matmul(
@@ -377,9 +377,9 @@ def tile_metalstmcell_pb_e_kernel(
         prepare_h(0, "a_ps")
         prepare_h(1, "a_ps")
         prepare_h(2, "w_ps")
-        prepare_h(3, "w_ps")
         prepare_gate_matrix("zh", 0, ("d_ps",))
         prepare_gate_matrix("dh", 0, ("d_ps", "a_ps"))
+        prepare_h(3, "w_ps")
 
         def on(k):
             return 0 <= k < UNITS
@@ -412,9 +412,10 @@ def tile_metalstmcell_pb_e_kernel(
                 cell_tanh(step - 5)
             if on(step + 2):
                 mx_matmuls(step + 2)
-            if step == -1:
-                prepare_gate_matrix("zb", 0, ("a_ps",), True)
+            if step == -2:
+                prepare_gate_matrix("zb", 0, ("a_ps",))
                 prepare_gate_matrix("db", 0, ("d_ps", "d_ps"))
+            if step == -1:
                 prepare_rows()
             if step == 0:
                 prepare_gate_matrix("dh", 1)
@@ -423,11 +424,10 @@ def tile_metalstmcell_pb_e_kernel(
                     prepare_gate_matrix(name, g + 1)
             if 0 <= g and g + 2 < G and bt == NBT - 1:
                 prepare_gate_matrix("dh", g + 2)
-            if 0 <= g < G and bt == 0:
-                spread_ln_row("lnw", g)
             if on(step + 1):
                 shift_matmuls(step + 1)
             if 0 <= g < G and bt == 0:
+                spread_ln_row("lnw", g)
                 spread_ln_row("lnb", g)
             if on(step - 3):
                 cell_sum(step - 3)

@@ -238,15 +238,17 @@ def tile_metalstmcell_pb_e_kernel(
             for half in range(HALVES):
                 cols = slice(half * BANK, (half + 1) * BANK)
                 d_ps = psum_m.tile([P, BANK], F32, tag="a_ps" if k == UNITS - 1 else "d_ps")
-                nc.tensor.matmul(d_ps[:], lhsT=ones[:], rhs=beta_rows[:, ORDER[g], cols], start=True, stop=False)
                 for e in range(2):
                     nc.tensor.matmul(
                         d_ps[:],
                         lhsT=gate_T[("zb", g)][:, bt * P : (bt + 1) * P, e],
                         rhs=gate_T[("db", g)][:, cols, e],
-                        start=False,
-                        stop=(e == 1 and g != PX_ON_TENSOR),
+                        start=(e == 0),
+                        stop=False,
                     )
+                nc.tensor.matmul(
+                    d_ps[:], lhsT=ones[:], rhs=beta_rows[:, ORDER[g], cols], start=False, stop=(g != PX_ON_TENSOR)
+                )
                 if g == PX_ON_TENSOR:
                     nc.tensor.matmul(
                         d_ps[:], lhsT=ident_bf16[:], rhs=gate_px[g][:, bt, cols], start=False, stop=True
@@ -354,14 +356,14 @@ def tile_metalstmcell_pb_e_kernel(
             if g == 2:
                 nc.scalar.activation(out=keep_a[:, bt, :], in_=keep_b[:, bt, :], func=ACT.Tanh)
 
-        for bt in range(NBT):
+        load_h(0)
+        load_scale_planes(0)
+        for bt in range(1, NBT):
             load_h(bt)
         load_gate_matrices(0, ("zh", "dh"))
-        load_scale_planes(0)
         load_gate_words(0)
-        load_gate_matrices(0, ("zb",))
+        load_gate_matrices(0, ("zb", "db"))
         load_px(0, 0)
-        load_gate_matrices(0, ("db",))
         nc.sync.dma_start(out=beta_rows[0:1, :, :], in_=db_b.rearrange("(o g) n -> o g n", o=1))
         load_rows()
         load_px(0, 1)
@@ -431,7 +433,7 @@ def tile_metalstmcell_pb_e_kernel(
                 spread_ln_row("lnb", g)
             if on(step - 3):
                 cell_sum(step - 3)
-                hidden(step - 3, nc.gpsimd if step < UNITS + 1 else nc.vector)
+                hidden(step - 3, nc.gpsimd if step < UNITS else nc.vector)
             if 0 <= g and g + 2 < G and bt == 0:
                 load_gate_matrices(g + 2, ("dh", "zh", "zb", "db"))
             if 1 <= g and g + 1 < G and bt == 0:

from contextlib import ExitStack

import concourse.mybir as mybir
from concourse.masks import make_identity

F32 = mybir.dt.float32
BF16 = mybir.dt.bfloat16
I32 = mybir.dt.int32
U32 = mybir.dt.uint32
U8 = mybir.dt.uint8
FP8X4 = mybir.dt.float8_e4m3fn_x4
ALU = mybir.AluOpType
ACT = mybir.ActivationFunctionType

P = 128
B, H, Z, G = 512, 1024, 256, 4
EPS = 1e-5
NBT = B // P
UNITS = G * NBT
BANK = 512
HALVES = H // BANK
K_PASS = 512
PASSES = H // K_PASS
PLANES = 4
QUARTERS = 4
MATRICES = ("dh", "zh", "db", "zb")
ROW_INDEX = {"lnw": 0, "lnb": 1}

FLOPS = 2 * B * G * H * (H + 2 * Z)

PX_ON_TENSOR = G - 1
GATE_FUNC = (ACT.Sigmoid, ACT.Sigmoid, ACT.Tanh, ACT.Sigmoid)
WEIGHTS = ("dh", "db")
ORDER = (1, 0, 2, 3)


def tile_metalstmcell_pb_e_kernel(
    tc, h, c, zh, zb, px, dh_w, db_w, db_b, w_h_words, w_h_scales, ln_w, ln_b, h_next, c_next
):
    nc = tc.nc
    with ExitStack() as ctx:
        ctx.enter_context(tc.manual_schedule())
        const = ctx.enter_context(tc.tile_pool(name="const", bufs=1))
        raw = ctx.enter_context(tc.tile_pool(name="raw", bufs=NBT))
        gatew = ctx.enter_context(tc.tile_pool(name="gatew", bufs=2))
        work = ctx.enter_context(tc.tile_pool(name="work", bufs=2))
        stats = ctx.enter_context(tc.tile_pool(name="stats", bufs=4))
        psum_m = ctx.enter_context(tc.psum_pool(name="psum_m", bufs=2))
        psum_ln = ctx.enter_context(tc.psum_pool(name="psum_ln", bufs=1))

        planes = const.tile([P, 8 // PLANES, H], U8, align_bytes=64)
        nc.vector.memset(planes[:].bitcast(I32), 0)
        ident_f32 = const.tile([P, P], F32)
        make_identity(nc, ident_f32[:])
        ident_bf16 = const.tile([P, P], BF16)
        make_identity(nc, ident_bf16[:])
        neg_half = const.tile([P, 1], F32)
        nc.gpsimd.memset(neg_half[:], -0.5)
        eps_col = const.tile([P, 1], F32)
        nc.gpsimd.memset(eps_col[:], EPS)

        warm = const.tile([P, 1], F32)
        nc.scalar.activation(out=warm[:], in_=eps_col[:], func=ACT.Sigmoid)

        rows_raw = const.tile([P, 2 * P], BF16)
        nc.vector.memset(rows_raw[:].bitcast(F32), 0.0)
        rowsT = const.tile([P, 2 * P], BF16)
        ones = const.tile([P, P], BF16)
        nc.vector.memset(ones[:], 1.0)
        beta_rows = const.tile([P, G, H], BF16)
        nc.vector.memset(beta_rows[:].bitcast(F32), 0.0)

        h_codes = const.tile([P, NBT, PASSES * P], U32, align_bytes=64)
        h_scales = const.tile([P, NBT, PASSES * P], U8, align_bytes=64)
        c_sb = const.tile([P, NBT, H], BF16)
        keep_a = const.tile([P, NBT, H], F32)
        keep_b = const.tile([P, NBT, H], F32)

        h_raws = {}
        gate_raw = {}
        gate_mx = {}
        gate_px = {}
        gate_rows = {}
        gate_T = {}
        banks = {}
        a_sbs, ts, ys, ysums, neg_mus, ssqs, rstds, vs = {}, {}, {}, {}, {}, {}, {}, {}

        def load_scale_planes(j):
            for q in range(4):
                nc.sync.dma_start(
                    out=planes[32 * q : 32 * q + 4 * PLANES, j, :].bitcast(I32),
                    in_=w_h_scales[PLANES * j : PLANES * (j + 1), 4 * q : 4 * q + 4, :].bitcast(I32),
                )

        def load_h(bt):
            h_raw = raw.tile([P, H], BF16, tag="h_raw")
            nc.sync.dma_start(out=h_raw[:], in_=h[bt * P : (bt + 1) * P, :])
            h_raws[bt] = h_raw

        def load_gate_matrices(g, names):
            real = ORDER[g]
            sources = {"dh": dh_w[real], "zh": zh[:, real, :], "db": db_w[real], "zb": zb[:, real, :]}
            for name in names:
                rows = sources[name]
                loaded = gatew.tile([P, rows.shape[0] // P, Z], BF16, tag=name + "_raw")
                if name in WEIGHTS:
                    nc.sync.dma_start(
                        out=loaded[:].rearrange("p (q t) z -> p q (t z)", t=4),
                        in_=rows.rearrange("(q p t) z -> p q (t z)", p=P, t=4),
                    )
                else:
                    nc.sync.dma_start(out=loaded[:], in_=rows.rearrange("(j p) z -> p j z", p=P))
                gate_raw[(name, g)] = loaded

        def load_gate_words(g):
            words = gatew.tile([P, PASSES, H], U32, tag="words", align_bytes=64)
            for half in range(HALVES):
                cols = slice(half * BANK, (half + 1) * BANK)
                nc.sync.dma_start(
                    out=words[:, :, cols].bitcast(I32),
                    in_=w_h_words[PASSES * ORDER[g] : PASSES * (ORDER[g] + 1), :, cols, :]
                    .rearrange("s p n t -> p s (n t)")
                    .bitcast(I32),
                )
            gate_mx[g] = words
            px_sb = gatew.tile([P, NBT, H], BF16, tag="px_sb")
            gate_px[g] = px_sb

        def load_px(g, bt):
            nc.sync.dma_start(out=gate_px[g][:, bt, :], in_=px[bt * P : (bt + 1) * P, ORDER[g], :])

        def load_rows():
            for i, vector in enumerate((ln_w, ln_b)):
                nc.sync.dma_start(
                    out=rows_raw[G * QUARTERS * i : G * QUARTERS * (i + 1), :],
                    in_=vector.rearrange("g (q w) -> (g q) w", q=QUARTERS),
                )

        def transpose_pairs(word_blocks, dst, tag, on_vector, interleaved):
            tp = psum_m.tile([P, 4, P], F32, tag=tag)
            for j in range(4):
                nc.tensor.transpose(tp[:, j, :], word_blocks[:, j, :], ident_f32[:])
            source = tp[:].rearrange("p t r -> p r t") if interleaved else tp[:]
            target = dst.bitcast(F32)
            if interleaved:
                target = target.rearrange("p t r -> p (t r)").rearrange("p (r t) -> p r t", t=4)
            if on_vector:
                nc.vector.tensor_copy(out=target, in_=source)
            else:
                nc.scalar.copy(out=target, in_=source)

        def prepare_rows():
            tp = psum_m.tile([P, 4, P], F32, tag="a_ps")
            nc.tensor.transpose(tp[:, 0, :], rows_raw[:].bitcast(F32), ident_f32[:])
            nc.scalar.copy(out=rowsT[:].bitcast(F32), in_=tp[:, 0, :])

        def spread_row(name, g, bank):
            for q in range(QUARTERS):
                r = G * QUARTERS * ROW_INDEX[name] + QUARTERS * ORDER[g] + q
                nc.tensor.transpose(
                    bank[:, q * P : (q + 1) * P],
                    rowsT[:].bitcast(F32)[:, r : r + 1].to_broadcast([P, P]),
                    ident_f32[:],
                )

        def spread_ln_row(name, g):
            bank = psum_ln.tile([P, BANK], F32, tag=name)
            spread_row(name, g, bank)
            gate_rows[(name, g)] = bank[:].bitcast(BF16)

        def prepare_h(bt, tag="a_ps"):
            h_words = h_raws[bt][:].bitcast(F32)
            tp = psum_m.tile([P, 4, P], F32, tag=tag)
            for s in range(PASSES):
                for u in range(2):
                    nc.tensor.transpose(
                        tp[:, 2 * s + u, :],
                        h_words[:, 256 * s + u : 256 * (s + 1) : 2],
                        ident_f32[:],
                    )
            grouped = raw.tile([P, PASSES, P, 4], BF16, tag="grouped", bufs=2, align_bytes=64)
            nc.vector.tensor_copy(
                out=grouped[:].bitcast(F32), in_=tp[:].rearrange("p (s u) b -> p s b u", u=2)
            )
            nc.vector.quantize_mx(
                out=h_codes[:, bt, :].bitcast(FP8X4),
                scales=h_scales[:, bt, :],
                in_=grouped[:].rearrange("p s b t -> p (s b t)"),
            )

        def prepare_gate_matrix(name, g, tags=("a_ps", "a_ps"), on_vector=False):
            src_words = gate_raw[(name, g)][:].bitcast(F32)
            blocks = src_words.shape[1]
            dst = gatew.tile([P, blocks * P, 2], BF16, tag=name + "T")
            dst_blocks = dst[:].rearrange("p (j r) e -> p j (r e)", r=P)
            for q in range(blocks // 4):
                transpose_pairs(src_words[:, 4 * q : 4 * q + 4, :], dst_blocks[:, 4 * q : 4 * q + 4, :], tags[q], on_vector, name in WEIGHTS)
            gate_T[(name, g)] = dst

        def scale_matmuls(k):
            g, bt = divmod(k, NBT)
            a_sb = work.tile([P, H], F32, tag="a_sb")
            for half in range(HALVES):
                cols = slice(half * BANK, (half + 1) * BANK)
                a_ps = psum_m.tile([P, BANK], F32, tag="a_ps")
                for e in range(2):
                    nc.tensor.matmul(
                        a_ps[:],
                        lhsT=gate_T[("zh", g)][:, bt * P : (bt + 1) * P, e],
                        rhs=gate_T[("dh", g)][:, cols, e],
                        start=(e == 0),
                        stop=(e == 1),
                    )
                nc.scalar.copy(out=a_sb[:, cols], in_=a_ps[:])
            a_sbs[k] = a_sb

        def mx_matmuls(k):
            g, bt = divmod(k, NBT)
            for half in range(HALVES):
                cols = slice(half * BANK, (half + 1) * BANK)
                w_ps = psum_m.tile([P, BANK], F32, tag="w_ps")
                for s in range(PASSES):
                    group = PASSES * ORDER[g] + s
                    row0 = 4 * (group % PLANES)
                    nc.tensor.matmul_mx(
                        out=w_ps[:],
                        lhsT=h_codes[:, bt, s * P : (s + 1) * P].bitcast(FP8X4),
                        lhsT_scale=h_scales[:, bt, s * P : (s + 1) * P],
                        rhs=gate_mx[g][:, s, cols].bitcast(FP8X4),
                        rhs_scale=planes[row0:P, group // PLANES, cols],
                        start=(s == 0),
                        stop=(s == PASSES - 1),
                    )
                banks[("w", k, half)] = w_ps

        def shift_matmuls(k):
            g, bt = divmod(k, NBT)
            for half in range(HALVES):
                cols = slice(half * BANK, (half + 1) * BANK)
                d_ps = psum_m.tile([P, BANK], F32, tag="a_ps" if k == UNITS - 1 else "d_ps")
                for e in range(2):
                    nc.tensor.matmul(
                        d_ps[:],
                        lhsT=gate_T[("zb", g)][:, bt * P : (bt + 1) * P, e],
                        rhs=gate_T[("db", g)][:, cols, e],
                        start=(e == 0),
                        stop=False,
                    )
                nc.tensor.matmul(
                    d_ps[:], lhsT=ones[:], rhs=beta_rows[:, ORDER[g], cols], start=False, stop=(g != PX_ON_TENSOR)
                )
                if g == PX_ON_TENSOR:
                    nc.tensor.matmul(
                        d_ps[:], lhsT=ident_bf16[:], rhs=gate_px[g][:, bt, cols], start=False, stop=True
                    )
                banks[("d", k, half)] = d_ps

        def multiply(k):
            t = work.tile([P, H], F32, tag="t")
            for half in reversed(range(HALVES)):
                cols = slice(half * BANK, (half + 1) * BANK)
                nc.vector.tensor_mul(out=t[:, cols], in0=a_sbs[k][:, cols], in1=banks[("w", k, half)][:])
            ts[k] = t

        def add_px(k):
            g, bt = divmod(k, NBT)
            if g != PX_ON_TENSOR:
                nc.gpsimd.tensor_tensor(out=ts[k][:], in0=ts[k][:], in1=gate_px[g][:, bt, :], op=ALU.add)

        def add_shift(k):
            y = work.tile([P, H], F32, tag="y")
            ysum = stats.tile([P, HALVES], F32, tag="ysum")
            for half in reversed(range(HALVES)):
                cols = slice(half * BANK, (half + 1) * BANK)
                nc.vector.scalar_tensor_tensor(
                    out=y[:, cols],
                    in0=ts[k][:, cols],
                    scalar=1.0,
                    in1=banks[("d", k, half)][:],
                    op0=ALU.mult,
                    op1=ALU.add,
                    accum_out=ysum[:, half : half + 1],
                )
            ys[k] = y
            ysums[k] = ysum

        def mean(k):
            junk2 = stats.tile([P, HALVES], F32, tag="junk2")
            neg_mu = stats.tile([P, 1], F32, tag="neg_mu")
            nc.scalar.activation(
                out=junk2[:], in_=ysums[k][:], func=ACT.Copy, scale=-1.0 / H, accum_out=neg_mu[:]
            )
            neg_mus[k] = neg_mu

        def squares(k):
            sq = work.tile([P, H], F32, tag="sq")
            ssq = stats.tile([P, 1], F32, tag="ssq")
            nc.scalar.activation(
                out=sq[:], in_=ys[k][:], func=ACT.Square, bias=neg_mus[k][:], scale=1.0, accum_out=ssq[:]
            )
            ssqs[k] = ssq

        def inverse_std(k):
            var_eps = stats.tile([P, 1], F32, tag="var_eps")
            nc.scalar.activation(out=var_eps[:], in_=ssqs[k][:], func=ACT.Identity, scale=1.0 / H, bias=eps_col[:])
            rstd = stats.tile([P, 1], F32, tag="rstd")
            nc.gpsimd.tensor_tensor(out=rstd[:], in0=var_eps[:], in1=neg_half[:], op=ALU.pow)
            rstds[k] = rstd

        def centre_and_gain(k):
            v = work.tile([P, H], F32, tag="v", bufs=5)
            nc.vector.scalar_tensor_tensor(
                out=v[:], in0=ys[k][:], scalar=neg_mus[k][:], in1=gate_rows[("lnw", k // NBT)],
                op0=ALU.add, op1=ALU.mult,
            )
            vs[k] = v

        def scale_and_shift(k):
            nc.vector.scalar_tensor_tensor(
                out=vs[k][:], in0=vs[k][:], scalar=rstds[k][:], in1=gate_rows[("lnb", k // NBT)],
                op0=ALU.mult, op1=ALU.add,
            )

        def activate(k):
            g, bt = divmod(k, NBT)
            g = ORDER[g]
            dst = {0: keep_a[:, bt, :], 1: keep_b[:, bt, :]}.get(g, vs[k][:])
            nc.scalar.activation(out=dst, in_=vs[k][:], func=GATE_FUNC[g])

        def cell(k):
            g, bt = divmod(k, NBT)
            g = ORDER[g]
            rows = slice(bt * P, (bt + 1) * P)
            if g == 2:
                nc.gpsimd.tensor_tensor(out=keep_a[:, bt, :], in0=keep_a[:, bt, :], in1=vs[k][:], op=ALU.mult)

        def forget(bt):
            nc.gpsimd.tensor_tensor(out=keep_b[:, bt, :], in0=keep_b[:, bt, :], in1=c_sb[:, bt, :], op=ALU.mult)

        def cell_sum(k):
            g, bt = divmod(k, NBT)
            g = ORDER[g]
            rows = slice(bt * P, (bt + 1) * P)
            if g == 2:
                nc.gpsimd.tensor_tensor(out=keep_b[:, bt, :], in0=keep_b[:, bt, :], in1=keep_a[:, bt, :], op=ALU.add)
                nc.sync.dma_start(out=c_next[rows, :], in_=keep_b[:, bt, :])

        def hidden(k, engine):
            g, bt = divmod(k, NBT)
            if g == 3:
                engine.tensor_tensor(out=vs[k][:], in0=vs[k][:], in1=keep_a[:, bt, :], op=ALU.mult)
                nc.sync.dma_start(out=h_next[bt * P : (bt + 1) * P, :], in_=vs[k][:])

        def cell_tanh(k):
            g, bt = divmod(k, NBT)
            if g == 2:
                nc.scalar.activation(out=keep_a[:, bt, :], in_=keep_b[:, bt, :], func=ACT.Tanh)

        load_h(0)
        load_scale_planes(0)
        for bt in range(1, NBT):
            load_h(bt)
        load_gate_matrices(0, ("zh", "dh"))
        load_gate_words(0)
        load_gate_matrices(0, ("zb", "db"))
        load_px(0, 0)
        nc.sync.dma_start(out=beta_rows[0:1, :, :], in_=db_b.rearrange("(o g) n -> o g n", o=1))
        load_rows()
        load_px(0, 1)
        load_px(0, 2)
        load_px(0, 3)
        load_gate_matrices(1, ("dh", "zh", "zb", "db"))
        nc.sync.dma_start(out=c_sb[:], in_=c.rearrange("(bt p) n -> p bt n", p=P))
        load_scale_planes(1)
        load_gate_words(1)
        for bt in range(NBT):
            load_px(1, bt)

        prepare_h(0, "a_ps")
        prepare_h(1, "a_ps")
        prepare_h(2, "w_ps")
        prepare_gate_matrix("zh", 0, ("d_ps",))
        prepare_gate_matrix("dh", 0, ("d_ps", "a_ps"))
        prepare_h(3, "w_ps")

        def on(k):
            return 0 <= k < UNITS

        for step in range(-2, UNITS + 4):
            g, bt = divmod(step, NBT)
            if on(step - 1):
                mean(step - 1)
                squares(step - 1)
            if on(step - 3):
                cell(step - 3)
            if 3 <= step < 3 + 2 * NBT and (step - 3) % 2 == 0:
                forget((step - 3) // 2)
            if on(step - 1):
                inverse_std(step - 1)
            if on(step + 1):
                multiply(step + 1)
                add_px(step + 1)
            if on(step - 1):
                centre_and_gain(step - 1)
            if on(step):
                add_shift(step)
            if on(step - 1):
                scale_and_shift(step - 1)
            if on(step + 2):
                scale_matmuls(step + 2)
            if on(step - 2):
                activate(step - 2)
            if on(step - 5):
                cell_tanh(step - 5)
            if on(step + 2):
                mx_matmuls(step + 2)
            if step == -2:
                prepare_gate_matrix("zb", 0, ("a_ps",))
                prepare_gate_matrix("db", 0, ("d_ps", "d_ps"))
            if step == -1:
                prepare_rows()
            if step == 0:
                prepare_gate_matrix("dh", 1)
            if 0 <= g and g + 1 < G:
                for name in ((), ("zh", "zb"), ("db",), ())[bt]:
                    prepare_gate_matrix(name, g + 1)
            if 0 <= g and g + 2 < G and bt == NBT - 1:
                prepare_gate_matrix("dh", g + 2)
            if on(step + 1):
                shift_matmuls(step + 1)
            if 0 <= g < G and bt == 0:
                spread_ln_row("lnw", g)
                spread_ln_row("lnb", g)
            if on(step - 3):
                cell_sum(step - 3)
                hidden(step - 3, nc.gpsimd if step < UNITS else nc.vector)
            if 0 <= g and g + 2 < G and bt == 0:
                load_gate_matrices(g + 2, ("dh", "zh", "zb", "db"))
            if 1 <= g and g + 1 < G and bt == 0:
                load_gate_words(g + 1)
                for later_bt in range(NBT):
                    load_px(g + 1, later_bt)
